import numpy as np
import ml_dtypes


def mxq(x, axis, fmt="e4m3"):
    dtype, down = {"e4m3": (ml_dtypes.float8_e4m3fn, 7), "e5m2": (ml_dtypes.float8_e5m2, 14)}[fmt]
    v = np.moveaxis(np.asarray(x, np.float32).astype(ml_dtypes.bfloat16).astype(np.float64), axis, -1)
    blocks = v.reshape(v.shape[:-1] + (-1, 32))
    amax = np.abs(blocks).max(-1, keepdims=True)
    byte = np.maximum(np.where(amax > 0, np.frexp(amax)[1] - 1 + 127, 0) - down, 1)
    scale = np.exp2(byte - 127.0)
    codes = (blocks / scale).astype(np.float32).astype(dtype).astype(np.float64)
    return np.moveaxis((codes * scale).reshape(v.shape), -1, axis)


WIDE = False


def mx_kscale(k):
    if not WIDE:
        return np.ones(k)
    levels = np.array([10, -10, 5, -5, 0])
    a = np.random.permutation(np.resize(levels, k // 512 * 4)).reshape(k // 512, 4)
    idx = np.arange(k)
    return np.exp2(a[idx // 512, idx % 128 // 32])


BF16 = ml_dtypes.bfloat16


def bf(x):
    return np.asarray(x, np.float32).astype(BF16)


def f64(x):
    return np.asarray(x).astype(np.float64)


B, I, HS, G = 8192, 1024, 128, 1
H = HS * G
MXK = 16 * 32
HH_MX = H % MXK == 0


def sigmoid(v):
    return 1.0 / (1.0 + np.exp(-v))


def setup_inputs():
    s = mx_kscale(I)
    t = mx_kscale(H) if HH_MX else np.ones(H)
    return {"input": bf(np.random.standard_normal((B, I)) * s),
            "h0": bf(np.random.standard_normal((B, H)) * t),
            "c0": bf(np.random.standard_normal((B, H))),
            "weight_ih": bf(np.random.standard_normal((I, 4 * H)) * 0.7 / np.sqrt(I) / s[:, None]),
            "weight_hh": bf(np.random.standard_normal((H, 4 * H)) * 0.7 / np.sqrt(H) / t[:, None]),
            "bias_ih": bf(np.random.standard_normal(4 * H) * 0.3),
            "bias_hh": bf(np.random.standard_normal(4 * H) * 0.3)}


def reference(input, h0, c0, weight_ih, weight_hh, bias_ih, bias_hh):
    pi = mxq(f64(input), 1, "e4m3") @ mxq(f64(weight_ih), 0, "e4m3")
    if HH_MX:
        ph = mxq(f64(h0), 1, "e4m3") @ mxq(f64(weight_hh), 0, "e4m3")
    else:
        ph = f64(h0) @ f64(weight_hh)
    gates = pi + f64(bias_ih) + ph + f64(bias_hh)
    c_in = f64(c0)
    h_parts, c_parts = [], []
    st = 0
    for _ in range(G):
        blk = gates[:, st * 4: st * 4 + 4 * HS]
        g, i, f, o = np.split(blk, 4, axis=-1)
        c1 = np.tanh(g) * sigmoid(i) + c_in[:, st: st + HS] * sigmoid(f)
        h_parts.append(np.tanh(c1) * sigmoid(o))
        c_parts.append(c1)
        st += HS
    return np.concatenate(h_parts, axis=-1), np.concatenate(c_parts, axis=-1)

@@ -1,0 +1,305 @@
+from contextlib import ExitStack
+
+import concourse.mybir as mybir
+from concourse.masks import make_identity
+
+F32 = mybir.dt.float32
+BF16 = mybir.dt.bfloat16
+U32 = mybir.dt.uint32
+U8 = mybir.dt.uint8
+FP8X4 = mybir.dt.float8_e4m3fn_x4
+ACT = mybir.ActivationFunctionType
+ALU = mybir.AluOpType
+
+P = 128
+BATCH = 8192
+K_IN = 1024
+HID = 128
+GATES = 512
+NT = BATCH // P
+GT = 2
+NG = NT // GT
+XC = 4
+XB = 5
+LEAD = 4
+MANUAL = True
+SMALL = ("g", "g", "g", "g")
+
+FLOPS = 2 * BATCH * K_IN * GATES + 2 * BATCH * HID * GATES
+
+
+def tile_symlstmcell_t_kernel(tc, x, h0, c0, weight_ih, weight_hh, bias_ih, bias_hh, out_0, out_1):
+    nc = tc.nc
+    xv = x.rearrange("(p t) k -> p t k", t=NT)
+    h0v = h0.rearrange("(p t) k -> p t k", t=NT)
+    c0v = c0.rearrange("(p t) k -> p t k", t=NT)
+    h1v = out_0.rearrange("(p t) u -> p t u", t=NT)
+    c1v = out_1.rearrange("(p t) u -> p t u", t=NT)
+
+    with ExitStack() as ctx:
+        const = ctx.enter_context(tc.tile_pool(name="const", bufs=1))
+        xpool = ctx.enter_context(tc.tile_pool(name="xpool", bufs=XB))
+        gpool = ctx.enter_context(tc.tile_pool(name="gpool", bufs=3))
+        qpool = ctx.enter_context(tc.tile_pool(name="qpool", bufs=3))
+        tpool = ctx.enter_context(tc.tile_pool(name="tpool", bufs=LEAD + 3))
+        apool = ctx.enter_context(tc.tile_pool(name="apool", bufs=3))
+        spool = ctx.enter_context(tc.tile_pool(name="spool", bufs=3))
+        opool = ctx.enter_context(tc.tile_pool(name="opool", bufs=3))
+        ps_x = ctx.enter_context(tc.psum_pool(name="ps_x", bufs=3))
+        ps_g = ctx.enter_context(tc.psum_pool(name="ps_g", bufs=2))
+        ps_p = ctx.enter_context(tc.psum_pool(name="ps_p", bufs=2))
+        ps_h = ctx.enter_context(tc.psum_pool(name="ps_h", bufs=1))
+        if MANUAL:
+            ctx.enter_context(tc.manual_schedule())
+
+        eng = {"v": nc.vector, "g": nc.gpsimd}
+
+        ident_f = const.tile([P, P], F32, name="ident_f")
+        ident_b = const.tile([P, P], BF16, name="ident_b")
+        make_identity(nc, ident_b[:])
+        make_identity(nc, ident_f[:])
+        ones = const.tile([P, P], BF16, name="ones")
+        nc.vector.memset(ones[:], 1.0)
+        btile = const.tile([P, GATES], BF16, name="btile")
+        nc.vector.memset(btile[:], 0.0)
+        warm = const.tile([P, 1], F32, name="warm")
+        nc.vector.memset(warm[:], 0.0)
+        nc.scalar.activation(out=warm[:], in_=warm[:], func=ACT.Sigmoid)
+
+        whh = const.tile([P, GATES], BF16, name="whh")
+        nc.sync.dma_start(out=whh[:], in_=weight_hh)
+        h0_parts = []
+        c0_parts = []
+
+        def load_part(parts, view, lo, hi, nm):
+            part = const.tile([P, hi - lo, HID], BF16, name="%s%d" % (nm, lo))
+            nc.sync.dma_start(out=part[:], in_=view[:, lo:hi, :])
+            parts.append((lo, hi, part))
+
+        def part_of(parts, lo, n):
+            found = [(a, part) for (a, b, part) in parts if a <= lo and lo + n <= b]
+            assert len(found) == 1
+            a, part = found[0]
+            return part[:, lo - a:lo - a + n, :]
+
+        load_part(h0_parts, h0v, 0, 8, "h0p")
+        nc.sync.dma_start(out=btile[0:1, :], in_=bias_ih.rearrange("(o n) -> o n", o=1))
+        nc.sync.dma_start(out=btile[1:2, :], in_=bias_hh.rearrange("(o n) -> o n", o=1))
+
+        xs = {}
+
+        def load_x(c):
+            xc = xpool.tile([P, XC, K_IN], BF16, name="xc")
+            nc.sync.dma_start(out=xc[:], in_=xv[:, XC * c:XC * (c + 1), :])
+            xs[c] = xc
+
+        w_raw = const.tile([P, 4 * K_IN], BF16, name="w_raw")
+        nc.sync.dma_start(
+            out=w_raw[:].rearrange("p (a r) -> p a r", a=4),
+            in_=weight_ih.rearrange("(a q e) c -> q a (e c)", a=4, e=2),
+        )
+        load_x(0)
+        load_x(1)
+        load_part(h0_parts, h0v, 8, 24, "h0p")
+        load_x(2)
+        load_part(c0_parts, c0v, 0, 16, "c0p")
+        load_x(3)
+        load_part(h0_parts, h0v, 24, NT, "h0p")
+        load_x(4)
+        load_part(c0_parts, c0v, 16, NT, "c0p")
+        for c in range(5, XB):
+            load_x(c)
+
+        hT = {}
+        xts = {}
+        grps = {}
+        cods = {}
+        scls = {}
+        ppss = {}
+        gpss = {}
+        tmps = {}
+        acts = {}
+        tcs = {}
+        c1os = {}
+        h1os = {}
+
+        h0ts = {}
+
+        def st_H(b):
+            h0t = ps_h.tile([P, 8, HID], BF16, name="h0t")
+            blk = part_of(h0_parts, 8 * b, 8)
+            for i in range(8):
+                nc.tensor.transpose(h0t[:, i, :], blk[:, i, :], ident_b[:])
+            h0ts[b] = h0t
+
+        def st_HC(b):
+            ht = const.tile([P, 8, HID], BF16, name="hT%d" % b)
+            nc.scalar.copy(out=ht[:], in_=h0ts[b][:])
+            hT[b] = ht
+
+        def st_P(j):
+            for jj in range(GT):
+                t = GT * j + jj
+                pps = ps_p.tile([P, GATES], F32, name="pps")
+                nc.tensor.matmul(out=pps[:], lhsT=hT[t // 8][:, t % 8, :], rhs=whh[:], start=True, stop=True)
+                ppss[t] = pps
+
+        def st_B(j):
+            tmp = tpool.tile([P, GT, GATES], F32, name="tmp")
+            for jj in range(GT):
+                nc.vector.tensor_tensor(out=tmp[:, jj, :], in0=ppss[GT * j + jj][:], in1=bias_bc[:], op=ALU.add)
+            tmps[j] = tmp
+
+        def st_T(j):
+            for jj in range(GT):
+                t = GT * j + jj
+                xt = ps_x.tile([P, 4, P], F32, name="xt")
+                xw = xs[t // XC][:, t % XC, :].bitcast(F32)
+                for u in range(4):
+                    nc.tensor.transpose(xt[:, u, :], xw[:, P * u:P * (u + 1)], ident_f[:])
+                xts[t] = xt
+            if j % 2 == 1 and j // 2 + XB < NT // XC:
+                load_x(j // 2 + XB)
+
+        def st_E(j):
+            grp = gpool.tile([P, GT, K_IN], BF16, name="grp", align_bytes=64)
+            for jj in range(GT):
+                nc.scalar.copy(
+                    out=grp[:, jj, :].bitcast(F32).rearrange("p (g b u) -> p g b u", g=2, u=2),
+                    in_=xts[GT * j + jj][:].rearrange("p (g u) b -> p g b u", u=2),
+                )
+            grps[j] = grp
+
+        def st_Q(j):
+            cod = qpool.tile([P, GT * 256], U32, name="cod", align_bytes=64)
+            scl = qpool.tile([P, GT * 256], U8, name="scl", align_bytes=64)
+            nc.vector.quantize_mx(
+                out=cod[:].bitcast(FP8X4), scales=scl[:], in_=grps[j][:].rearrange("p j c -> p (j c)")
+            )
+            cods[j] = cod
+            scls[j] = scl
+
+        def st_M(j):
+            for jj in range(GT):
+                gps = ps_g.tile([P, GATES], F32, name="gps")
+                for g in range(2):
+                    lo = jj * 256 + g * P
+                    nc.tensor.matmul_mx(
+                        out=gps[:],
+                        lhsT=cods[j][:, lo:lo + P].bitcast(FP8X4),
+                        lhsT_scale=scls[j][:, lo:lo + P],
+                        rhs=wq[:, g, :].bitcast(FP8X4),
+                        rhs_scale=ws[:, g, :],
+                        start=(g == 0),
+                        stop=(g == 1),
+                    )
+                gpss[GT * j + jj] = gps
+
+        def st_A(j):
+            for jj in range(GT):
+                nc.vector.tensor_tensor(
+                    out=tmps[j][:, jj, :], in0=gpss[GT * j + jj][:], in1=tmps[j][:, jj, :], op=ALU.add
+                )
+
+        def st_S1(j):
+            act = apool.tile([P, GT, GATES], F32, name="act")
+            nc.scalar.activation(out=act[:, :, HID:GATES], in_=tmps[j][:, :, HID:GATES], func=ACT.Sigmoid)
+            nc.scalar.activation(out=act[:, :, 0:HID], in_=tmps[j][:, :, 0:HID], func=ACT.Tanh)
+            acts[j] = act
+
+        def st_G1(j):
+            q = j // 2
+            if j % 2 == 0:
+                c1o = opool.tile([P, 2 * GT, HID], F32, name="c1o")
+                c1os[q] = c1o
+            act = acts[j]
+            lo = GT * (j % 2)
+            m1 = spool.tile([P, GT, HID], F32, name="m1")
+            m2 = spool.tile([P, GT, HID], F32, name="m2")
+            eng[SMALL[0]].tensor_tensor(out=m1[:], in0=act[:, :, 0:HID], in1=act[:, :, HID:2 * HID], op=ALU.mult)
+            eng[SMALL[1]].tensor_tensor(
+                out=m2[:], in0=act[:, :, 2 * HID:3 * HID], in1=part_of(c0_parts, GT * j, GT), op=ALU.mult
+            )
+            eng[SMALL[2]].tensor_tensor(out=c1os[q][:, lo:lo + GT, :], in0=m1[:], in1=m2[:], op=ALU.add)
+
+        def st_S2(j):
+            tc1 = spool.tile([P, GT, HID], F32, name="tc1")
+            lo = GT * (j % 2)
+            nc.scalar.activation(out=tc1[:], in_=c1os[j // 2][:, lo:lo + GT, :], func=ACT.Tanh)
+            tcs[j] = tc1
+
+        def st_G2(j):
+            q = j // 2
+            if j % 2 == 0:
+                h1o = opool.tile([P, 2 * GT, HID], F32, name="h1o")
+                h1os[q] = h1o
+            lo = GT * (j % 2)
+            eng[SMALL[3]].tensor_tensor(
+                out=h1os[q][:, lo:lo + GT, :], in0=tcs[j][:], in1=acts[j][:, :, 3 * HID:GATES], op=ALU.mult
+            )
+            if j % 2 == 1:
+                nc.sync.dma_start(out=c1v[:, 4 * q:4 * q + 4, :], in_=c1os[q][:])
+                nc.sync.dma_start(out=h1v[:, 4 * q:4 * q + 4, :], in_=h1os[q][:])
+
+        st_H(0)
+        st_HC(0)
+        bps = ps_p.tile([P, GATES], F32, name="pps")
+        nc.tensor.matmul(out=bps[:], lhsT=ones[:], rhs=btile[:], start=True, stop=True)
+        bias_bc = const.tile([P, GATES], F32, name="bias_bc")
+        nc.vector.tensor_copy(out=bias_bc[:], in_=bps[:])
+        st_P(0)
+        st_B(0)
+        st_P(1)
+        st_B(1)
+
+        wview = w_raw[:].rearrange("p (g t c) -> p g t c", g=2, t=4)
+        wq = const.tile([P, 2, GATES], U32, name="wq", align_bytes=64)
+        ws = const.tile([P, 2, GATES], U8, name="ws", align_bytes=64)
+        wg0 = const.tile([P, GATES, 4], BF16, name="wg0", align_bytes=64)
+        wg1 = const.tile([P, GATES, 4], BF16, name="wg1", align_bytes=64)
+        nc.vector.tensor_copy(out=wg0[:], in_=wview[:, 0].rearrange("p t c -> p c t"))
+        nc.vector.tensor_copy(out=wg1[:], in_=wview[:, 1].rearrange("p t c -> p c t"))
+        nc.vector.quantize_mx(out=wq[:, 0, :].bitcast(FP8X4), scales=ws[:, 0, :], in_=wg0[:].rearrange("p c t -> p (c t)"))
+        nc.vector.quantize_mx(out=wq[:, 1, :].bitcast(FP8X4), scales=ws[:, 1, :], in_=wg1[:].rearrange("p c t -> p (c t)"))
+        st_T(0)
+        st_E(0)
+        st_T(1)
+        st_E(1)
+        st_Q(0)
+        st_T(2)
+        st_E(2)
+        st_Q(1)
+        st_H(1)
+        st_HC(1)
+        for j in range(2, LEAD):
+            st_P(j)
+            st_B(j)
+
+        for i in range(0, NG + 3):
+            if i < NG:
+                st_M(i)
+                st_A(i)
+            jp = i + LEAD
+            hb = (jp + 1) // 4
+            new_h = (jp + 1) % 4 == 0 and jp + 1 < NG
+            if jp < NG:
+                st_P(jp)
+                st_B(jp)
+            if new_h:
+                st_H(hb)
+            if i + 3 < NG:
+                st_T(i + 3)
+            if i + 2 < NG:
+                st_Q(i + 2)
+            if 0 <= i - 1 < NG:
+                st_S1(i - 1)
+            if 0 <= i - 2 < NG:
+                st_S2(i - 2)
+            if new_h:
+                st_HC(hb)
+            if i + 3 < NG:
+                st_E(i + 3)
+            if 0 <= i - 1 < NG:
+                st_G1(i - 1)
+            if 0 <= i - 2 < NG:
+                st_G2(i - 2)

@@ -20,10 +20,22 @@ NT = BATCH // P
 GT = 2
 NG = NT // GT
 XC = 4
-XB = 5
+XB = 4
 LEAD = 4
 MANUAL = True
-SMALL = ("g", "g", "g", "g")
+SMALL = ("g", "g", "g", "v")
+EB = 2
+TAILB = 2
+SMALL_TAIL = ("v", "v", "v", "v")
+SB_SET = (3,)
+SB_MOD = 4
+QHEAD = 2
+TL = 5
+QL = 3
+D2 = 2
+D3 = 3
+HEADB = (1, 1, 1, 1)
+LINKB = 2
 
 FLOPS = 2 * BATCH * K_IN * GATES + 2 * BATCH * HID * GATES
 
@@ -39,12 +51,12 @@ def tile_symlstmcell_t_kernel(tc, x, h0, c0, weight_ih, weight_hh, bias_ih, bias
     with ExitStack() as ctx:
         const = ctx.enter_context(tc.tile_pool(name="const", bufs=1))
         xpool = ctx.enter_context(tc.tile_pool(name="xpool", bufs=XB))
-        gpool = ctx.enter_context(tc.tile_pool(name="gpool", bufs=3))
+        gpool = ctx.enter_context(tc.tile_pool(name="gpool", bufs=2))
         qpool = ctx.enter_context(tc.tile_pool(name="qpool", bufs=3))
         tpool = ctx.enter_context(tc.tile_pool(name="tpool", bufs=LEAD + 3))
-        apool = ctx.enter_context(tc.tile_pool(name="apool", bufs=3))
-        spool = ctx.enter_context(tc.tile_pool(name="spool", bufs=3))
-        opool = ctx.enter_context(tc.tile_pool(name="opool", bufs=3))
+        apool = ctx.enter_context(tc.tile_pool(name="apool", bufs=4))
+        opool = ctx.enter_context(tc.tile_pool(name="opool", bufs=4))
+        lpool = ctx.enter_context(tc.tile_pool(name="lpool", bufs=1))
         ps_x = ctx.enter_context(tc.psum_pool(name="ps_x", bufs=3))
         ps_g = ctx.enter_context(tc.psum_pool(name="ps_g", bufs=2))
         ps_p = ctx.enter_context(tc.psum_pool(name="ps_p", bufs=2))
@@ -58,16 +70,17 @@ def tile_symlstmcell_t_kernel(tc, x, h0, c0, weight_ih, weight_hh, bias_ih, bias
         ident_b = const.tile([P, P], BF16, name="ident_b")
         make_identity(nc, ident_b[:])
         make_identity(nc, ident_f[:])
-        ones = const.tile([P, P], BF16, name="ones")
-        nc.vector.memset(ones[:], 1.0)
         btile = const.tile([P, GATES], BF16, name="btile")
         nc.vector.memset(btile[:], 0.0)
+        ones = const.tile([P, P], BF16, name="ones")
+        nc.vector.memset(ones[:], 1.0)
         warm = const.tile([P, 1], F32, name="warm")
         nc.vector.memset(warm[:], 0.0)
+
+        nc.scalar.dma_start(out=btile[0:1, :], in_=bias_ih.rearrange("(o n) -> o n", o=1))
+        nc.scalar.dma_start(out=btile[1:2, :], in_=bias_hh.rearrange("(o n) -> o n", o=1))
         nc.scalar.activation(out=warm[:], in_=warm[:], func=ACT.Sigmoid)
 
-        whh = const.tile([P, GATES], BF16, name="whh")
-        nc.sync.dma_start(out=whh[:], in_=weight_hh)
         h0_parts = []
         c0_parts = []
 
@@ -82,10 +95,6 @@ def tile_symlstmcell_t_kernel(tc, x, h0, c0, weight_ih, weight_hh, bias_ih, bias
             a, part = found[0]
             return part[:, lo - a:lo - a + n, :]
 
-        load_part(h0_parts, h0v, 0, 8, "h0p")
-        nc.sync.dma_start(out=btile[0:1, :], in_=bias_ih.rearrange("(o n) -> o n", o=1))
-        nc.sync.dma_start(out=btile[1:2, :], in_=bias_hh.rearrange("(o n) -> o n", o=1))
-
         xs = {}
 
         def load_x(c):
@@ -93,6 +102,9 @@ def tile_symlstmcell_t_kernel(tc, x, h0, c0, weight_ih, weight_hh, bias_ih, bias
             nc.sync.dma_start(out=xc[:], in_=xv[:, XC * c:XC * (c + 1), :])
             xs[c] = xc
 
+        load_part(h0_parts, h0v, 0, 16, "h0p")
+        whh = const.tile([P, GATES], BF16, name="whh")
+        nc.sync.dma_start(out=whh[:], in_=weight_hh)
         w_raw = const.tile([P, 4 * K_IN], BF16, name="w_raw")
         nc.sync.dma_start(
             out=w_raw[:].rearrange("p (a r) -> p a r", a=4),
@@ -100,17 +112,16 @@ def tile_symlstmcell_t_kernel(tc, x, h0, c0, weight_ih, weight_hh, bias_ih, bias
         )
         load_x(0)
         load_x(1)
-        load_part(h0_parts, h0v, 8, 24, "h0p")
-        load_x(2)
         load_part(c0_parts, c0v, 0, 16, "c0p")
+        load_x(2)
+        load_part(h0_parts, h0v, 16, NT, "h0p")
         load_x(3)
-        load_part(h0_parts, h0v, 24, NT, "h0p")
-        load_x(4)
         load_part(c0_parts, c0v, 16, NT, "c0p")
-        for c in range(5, XB):
+        for c in range(4, XB):
             load_x(c)
 
         hT = {}
+        h0ts = {}
         xts = {}
         grps = {}
         cods = {}
@@ -118,12 +129,22 @@ def tile_symlstmcell_t_kernel(tc, x, h0, c0, weight_ih, weight_hh, bias_ih, bias
         ppss = {}
         gpss = {}
         tmps = {}
-        acts = {}
-        tcs = {}
-        c1os = {}
-        h1os = {}
 
-        h0ts = {}
+        batches = []
+        j0 = 0
+        while j0 < NG:
+            n = EB if j0 + EB <= NG - TAILB else 1
+            batches.append((j0, n, SMALL if n == EB else SMALL_TAIL))
+            j0 += n
+        batch_of = {}
+        for bi, (bj, bn, be) in enumerate(batches):
+            for j in range(bj, bj + bn):
+                batch_of[j] = bi
+        acts = {}
+        c1os = {}
+
+        def on_scalar(t):
+            return t % SB_MOD in SB_SET
 
         def st_H(b):
             h0t = ps_h.tile([P, 8, HID], BF16, name="h0t")
@@ -141,14 +162,23 @@ def tile_symlstmcell_t_kernel(tc, x, h0, c0, weight_ih, weight_hh, bias_ih, bias
             for jj in range(GT):
                 t = GT * j + jj
                 pps = ps_p.tile([P, GATES], F32, name="pps")
-                nc.tensor.matmul(out=pps[:], lhsT=hT[t // 8][:, t % 8, :], rhs=whh[:], start=True, stop=True)
+                sc = on_scalar(t)
+                nc.tensor.matmul(out=pps[:], lhsT=hT[t // 8][:, t % 8, :], rhs=whh[:], start=True, stop=not sc)
+                if sc:
+                    nc.tensor.matmul(out=pps[:], lhsT=ones[:], rhs=btile[:], start=False, stop=True)
                 ppss[t] = pps
 
-        def st_B(j):
+        def st_BV(j):
             tmp = tpool.tile([P, GT, GATES], F32, name="tmp")
-            for jj in range(GT):
-                nc.vector.tensor_tensor(out=tmp[:, jj, :], in0=ppss[GT * j + jj][:], in1=bias_bc[:], op=ALU.add)
             tmps[j] = tmp
+            for jj in range(GT):
+                if not on_scalar(GT * j + jj):
+                    nc.vector.tensor_tensor(out=tmp[:, jj, :], in0=ppss[GT * j + jj][:], in1=bias_bc[:], op=ALU.add)
+
+        def st_BS(j):
+            for jj in range(GT):
+                if on_scalar(GT * j + jj):
+                    nc.scalar.copy(out=tmps[j][:, jj, :], in_=ppss[GT * j + jj][:])
 
         def st_T(j):
             for jj in range(GT):
@@ -161,23 +191,34 @@ def tile_symlstmcell_t_kernel(tc, x, h0, c0, weight_ih, weight_hh, bias_ih, bias
             if j % 2 == 1 and j // 2 + XB < NT // XC:
                 load_x(j // 2 + XB)
 
+        qb_of = {}
+        for j in range(NG):
+            if j < QHEAD:
+                qb_of[j] = (j, 1)
+            else:
+                qb_of[j] = (j - (j - QHEAD) % 2, 2)
+
         def st_E(j):
-            grp = gpool.tile([P, GT, K_IN], BF16, name="grp", align_bytes=64)
+            f, n = qb_of[j]
+            if j == f:
+                grp = gpool.tile([P, n * GT, K_IN], BF16, name="grp", align_bytes=64)
+                grps[f] = grp
             for jj in range(GT):
                 nc.scalar.copy(
-                    out=grp[:, jj, :].bitcast(F32).rearrange("p (g b u) -> p g b u", g=2, u=2),
+                    out=grps[f][:, (j - f) * GT + jj, :].bitcast(F32).rearrange("p (g b u) -> p g b u", g=2, u=2),
                     in_=xts[GT * j + jj][:].rearrange("p (g u) b -> p g b u", u=2),
                 )
-            grps[j] = grp
 
-        def st_Q(j):
-            cod = qpool.tile([P, GT * 256], U32, name="cod", align_bytes=64)
-            scl = qpool.tile([P, GT * 256], U8, name="scl", align_bytes=64)
+        def st_Q(f):
+            n = qb_of[f][1]
+            cod = qpool.tile([P, n * GT * 256], U32, name="cod", align_bytes=64)
+            scl = qpool.tile([P, n * GT * 256], U8, name="scl", align_bytes=64)
             nc.vector.quantize_mx(
-                out=cod[:].bitcast(FP8X4), scales=scl[:], in_=grps[j][:].rearrange("p j c -> p (j c)")
+                out=cod[:].bitcast(FP8X4), scales=scl[:], in_=grps[f][:].rearrange("p j c -> p (j c)")
             )
-            cods[j] = cod
-            scls[j] = scl
+            for j in range(f, f + n):
+                cods[j] = cod[:, (j - f) * GT * 256:(j - f + 1) * GT * 256]
+                scls[j] = scl[:, (j - f) * GT * 256:(j - f + 1) * GT * 256]
 
         def st_M(j):
             for jj in range(GT):
@@ -202,44 +243,55 @@ def tile_symlstmcell_t_kernel(tc, x, h0, c0, weight_ih, weight_hh, bias_ih, bias
                 )
 
         def st_S1(j):
-            act = apool.tile([P, GT, GATES], F32, name="act")
+            bi = batch_of[j]
+            bj, bn, be = batches[bi]
+            if j == bj:
+                act = apool.tile([P, bn * GT, GATES], F32, name="act")
+                acts[bi] = act
+            lo = (j - bj) * GT
+            act = acts[bi][:, lo:lo + GT, :]
             nc.scalar.activation(out=act[:, :, HID:GATES], in_=tmps[j][:, :, HID:GATES], func=ACT.Sigmoid)
             nc.scalar.activation(out=act[:, :, 0:HID], in_=tmps[j][:, :, 0:HID], func=ACT.Tanh)
-            acts[j] = act
 
-        def st_G1(j):
-            q = j // 2
-            if j % 2 == 0:
-                c1o = opool.tile([P, 2 * GT, HID], F32, name="c1o")
-                c1os[q] = c1o
-            act = acts[j]
-            lo = GT * (j % 2)
-            m1 = spool.tile([P, GT, HID], F32, name="m1")
-            m2 = spool.tile([P, GT, HID], F32, name="m2")
-            eng[SMALL[0]].tensor_tensor(out=m1[:], in0=act[:, :, 0:HID], in1=act[:, :, HID:2 * HID], op=ALU.mult)
-            eng[SMALL[1]].tensor_tensor(
-                out=m2[:], in0=act[:, :, 2 * HID:3 * HID], in1=part_of(c0_parts, GT * j, GT), op=ALU.mult
+        tcbs = {}
+
+        def link_tile(bn):
+            if bn == EB:
+                lk = lpool.tile([P, bn * GT, HID], F32, name="lk", bufs=LINKB)
+            else:
+                lk = lpool.tile([P, bn * GT, HID], F32, name="lkt", bufs=2)
+            return lk
+
+        def st_G1(bi):
+            bj, bn, be = batches[bi]
+            act = acts[bi]
+            c1o = opool.tile([P, bn * GT, HID], F32, name="c1o")
+            c1os[bi] = c1o
+            m1 = link_tile(bn)
+            tcbs[bi] = m1
+            eng[be[0]].tensor_tensor(out=m1[:], in0=act[:, :, 0:HID], in1=act[:, :, HID:2 * HID], op=ALU.mult)
+            eng[be[1]].tensor_tensor(
+                out=act[:, :, 2 * HID:3 * HID], in0=act[:, :, 2 * HID:3 * HID],
+                in1=part_of(c0_parts, GT * bj, GT * bn), op=ALU.mult
             )
-            eng[SMALL[2]].tensor_tensor(out=c1os[q][:, lo:lo + GT, :], in0=m1[:], in1=m2[:], op=ALU.add)
+            eng[be[2]].tensor_tensor(out=c1o[:], in0=m1[:], in1=act[:, :, 2 * HID:3 * HID], op=ALU.add)
+            nc.sync.dma_start(out=c1v[:, GT * bj:GT * (bj + bn), :], in_=c1o[:])
 
-        def st_S2(j):
-            tc1 = spool.tile([P, GT, HID], F32, name="tc1")
-            lo = GT * (j % 2)
-            nc.scalar.activation(out=tc1[:], in_=c1os[j // 2][:, lo:lo + GT, :], func=ACT.Tanh)
-            tcs[j] = tc1
+        def st_S2(bi):
+            bj, bn, be = batches[bi]
+            nc.scalar.activation(out=tcbs[bi][:], in_=c1os[bi][:], func=ACT.Tanh)
 
-        def st_G2(j):
-            q = j // 2
-            if j % 2 == 0:
-                h1o = opool.tile([P, 2 * GT, HID], F32, name="h1o")
-                h1os[q] = h1o
-            lo = GT * (j % 2)
-            eng[SMALL[3]].tensor_tensor(
-                out=h1os[q][:, lo:lo + GT, :], in0=tcs[j][:], in1=acts[j][:, :, 3 * HID:GATES], op=ALU.mult
-            )
-            if j % 2 == 1:
-                nc.sync.dma_start(out=c1v[:, 4 * q:4 * q + 4, :], in_=c1os[q][:])
-                nc.sync.dma_start(out=h1v[:, 4 * q:4 * q + 4, :], in_=h1os[q][:])
+        def st_G2(bi):
+            bj, bn, be = batches[bi]
+            act = acts[bi]
+            h1o = opool.tile([P, bn * GT, HID], F32, name="h1o")
+            eng[be[3]].tensor_tensor(out=h1o[:], in0=tcbs[bi][:], in1=act[:, :, 3 * HID:GATES], op=ALU.mult)
+            nc.sync.dma_start(out=h1v[:, GT * bj:GT * (bj + bn), :], in_=h1o[:])
+
+        def plain(j):
+            st_P(j)
+            st_BV(j)
+            st_BS(j)
 
         st_H(0)
         st_HC(0)
@@ -247,59 +299,115 @@ def tile_symlstmcell_t_kernel(tc, x, h0, c0, weight_ih, weight_hh, bias_ih, bias
         nc.tensor.matmul(out=bps[:], lhsT=ones[:], rhs=btile[:], start=True, stop=True)
         bias_bc = const.tile([P, GATES], F32, name="bias_bc")
         nc.vector.tensor_copy(out=bias_bc[:], in_=bps[:])
-        st_P(0)
-        st_B(0)
-        st_P(1)
-        st_B(1)
+        st_H(1)
+        st_HC(1)
+        nb = 0
+        for j in range(HEADB[0]):
+            plain(nb)
+            nb += 1
 
         wview = w_raw[:].rearrange("p (g t c) -> p g t c", g=2, t=4)
         wq = const.tile([P, 2, GATES], U32, name="wq", align_bytes=64)
         ws = const.tile([P, 2, GATES], U8, name="ws", align_bytes=64)
         wg0 = const.tile([P, GATES, 4], BF16, name="wg0", align_bytes=64)
         wg1 = const.tile([P, GATES, 4], BF16, name="wg1", align_bytes=64)
-        nc.vector.tensor_copy(out=wg0[:], in_=wview[:, 0].rearrange("p t c -> p c t"))
-        nc.vector.tensor_copy(out=wg1[:], in_=wview[:, 1].rearrange("p t c -> p c t"))
+        nc.vector.tensor_copy(
+            out=wg0[:].rearrange("p (c i) t -> p c t i", i=4), in_=wview[:, 0].rearrange("p t (c i) -> p c t i", i=4)
+        )
+        nc.scalar.copy(
+            out=wg1[:].rearrange("p (c i) t -> p c t i", i=4), in_=wview[:, 1].rearrange("p t (c i) -> p c t i", i=4)
+        )
+        for j in range(HEADB[1]):
+            plain(nb)
+            nb += 1
         nc.vector.quantize_mx(out=wq[:, 0, :].bitcast(FP8X4), scales=ws[:, 0, :], in_=wg0[:].rearrange("p c t -> p (c t)"))
         nc.vector.quantize_mx(out=wq[:, 1, :].bitcast(FP8X4), scales=ws[:, 1, :], in_=wg1[:].rearrange("p c t -> p (c t)"))
         st_T(0)
         st_E(0)
         st_T(1)
         st_E(1)
+        for j in range(HEADB[2]):
+            plain(nb)
+            nb += 1
         st_Q(0)
-        st_T(2)
-        st_E(2)
+        for j in range(HEADB[3]):
+            plain(nb)
+            nb += 1
         st_Q(1)
-        st_H(1)
-        st_HC(1)
-        for j in range(2, LEAD):
-            st_P(j)
-            st_B(j)
+        assert nb <= LEAD
 
-        for i in range(0, NG + 3):
-            if i < NG:
-                st_M(i)
-                st_A(i)
-            jp = i + LEAD
-            hb = (jp + 1) // 4
-            new_h = (jp + 1) % 4 == 0 and jp + 1 < NG
-            if jp < NG:
-                st_P(jp)
-                st_B(jp)
-            if new_h:
-                st_H(hb)
-            if i + 3 < NG:
-                st_T(i + 3)
-            if i + 2 < NG:
-                st_Q(i + 2)
-            if 0 <= i - 1 < NG:
-                st_S1(i - 1)
-            if 0 <= i - 2 < NG:
-                st_S2(i - 2)
-            if new_h:
+        NK = NG // 2
+        assert nb == LEAD
+
+        def plain_pe_v(j, first, count):
+            if j < NG:
+                st_P(j)
+                st_BV(j)
+
+        def maybe_H(j):
+            if j < NG and (j + 1) % 4 == 0 and j + 1 < NG and (j + 1) // 4 >= 2:
+                st_H((j + 1) // 4)
+                return [(j + 1) // 4]
+            return []
+
+        n_full = len([b for b in batches if b[1] == EB])
+        for k in range(0, NK + 4):
+            i0 = 2 * k
+            i1 = 2 * k + 1
+            if 0 <= i0 - 1 < NG and batches[batch_of[i0 - 1]][1] == EB:
+                st_S1(i0 - 1)
+            if 2 <= k + 1 < NK:
+                st_Q(2 * (k + 1))
+            if 0 <= k - 3 < n_full:
+                st_G2(k - 3)
+            if 0 <= k - 1 < n_full:
+                st_G1(k - 1)
+            if k >= NK:
+                if 0 <= k - 2 < n_full:
+                    st_S2(k - 2)
+                continue
+            g0 = i0 + LEAD
+            g1 = i1 + LEAD
+            st_M(i0)
+            st_A(i0)
+            if k == 0:
+                st_T(2)
+                st_E(2)
+            elif i0 + 4 < NG:
+                st_T(i0 + 4)
+                st_E(i0 + 4)
+            plain_pe_v(g0, 0, 2)
+            if g0 < NG:
+                st_BS(g0)
+            hs = maybe_H(g0)
+            single = batches[batch_of[i0]][1] == 1
+            if 0 <= k - 2 < n_full:
+                st_S2(k - 2)
+            st_S1(i0)
+            st_M(i1)
+            st_A(i1)
+            if single:
+                st_G1(batch_of[i0])
+                st_S2(batch_of[i0])
+                st_S1(i1)
+                st_G1(batch_of[i1])
+                st_G2(batch_of[i0])
+                st_S2(batch_of[i1])
+                st_G2(batch_of[i1])
+            if k == 0:
+                st_T(3)
+                st_E(3)
+                st_Q(2)
+                st_T(4)
+                st_E(4)
+                st_T(5)
+                st_E(5)
+            elif i1 + 4 < NG:
+                st_T(i1 + 4)
+                st_E(i1 + 4)
+            plain_pe_v(g1, 0, 2)
+            if g1 < NG:
+                st_BS(g1)
+            hs = hs + maybe_H(g1)
+            for hb in hs:
                 st_HC(hb)
-            if i + 3 < NG:
-                st_E(i + 3)
-            if 0 <= i - 1 < NG:
-                st_G1(i - 1)
-            if 0 <= i - 2 < NG:
-                st_G2(i - 2)

@@ -23,12 +23,12 @@ XC = 4
 XB = 4
 LEAD = 4
 MANUAL = True
-SMALL = ("g", "g", "g", "v")
+SMALL = ("g", "g", "v", "v")
 EB = 2
 TAILB = 2
 SMALL_TAIL = ("v", "v", "v", "v")
-SB_SET = (3,)
-SB_MOD = 4
+SB_SET = (3, 5, 7)
+SB_MOD = 8
 QHEAD = 2
 TL = 5
 QL = 3
@@ -36,6 +36,7 @@ D2 = 2
 D3 = 3
 HEADB = (1, 1, 1, 1)
 LINKB = 2
+CL = 2
 
 FLOPS = 2 * BATCH * K_IN * GATES + 2 * BATCH * HID * GATES
 
@@ -77,7 +78,7 @@ def tile_symlstmcell_t_kernel(tc, x, h0, c0, weight_ih, weight_hh, bias_ih, bias
         warm = const.tile([P, 1], F32, name="warm")
         nc.vector.memset(warm[:], 0.0)
 
-        nc.scalar.dma_start(out=btile[0:1, :], in_=bias_ih.rearrange("(o n) -> o n", o=1))
+        nc.sync.dma_start(out=btile[0:1, :], in_=bias_ih.rearrange("(o n) -> o n", o=1))
         nc.scalar.dma_start(out=btile[1:2, :], in_=bias_hh.rearrange("(o n) -> o n", o=1))
         nc.scalar.activation(out=warm[:], in_=warm[:], func=ACT.Sigmoid)
 
@@ -274,7 +275,11 @@ def tile_symlstmcell_t_kernel(tc, x, h0, c0, weight_ih, weight_hh, bias_ih, bias
                 out=act[:, :, 2 * HID:3 * HID], in0=act[:, :, 2 * HID:3 * HID],
                 in1=part_of(c0_parts, GT * bj, GT * bn), op=ALU.mult
             )
-            eng[be[2]].tensor_tensor(out=c1o[:], in0=m1[:], in1=act[:, :, 2 * HID:3 * HID], op=ALU.add)
+
+        def st_C1(bi):
+            bj, bn, be = batches[bi]
+            c1o = c1os[bi]
+            eng[be[2]].tensor_tensor(out=c1o[:], in0=tcbs[bi][:], in1=acts[bi][:, :, 2 * HID:3 * HID], op=ALU.add)
             nc.sync.dma_start(out=c1v[:, GT * bj:GT * (bj + bn), :], in_=c1o[:])
 
         def st_S2(bi):
@@ -358,6 +363,8 @@ def tile_symlstmcell_t_kernel(tc, x, h0, c0, weight_ih, weight_hh, bias_ih, bias
                 st_S1(i0 - 1)
             if 2 <= k + 1 < NK:
                 st_Q(2 * (k + 1))
+            if 0 <= k - CL < n_full:
+                st_C1(k - CL)
             if 0 <= k - 3 < n_full:
                 st_G2(k - 3)
             if 0 <= k - 1 < n_full:
@@ -388,9 +395,11 @@ def tile_symlstmcell_t_kernel(tc, x, h0, c0, weight_ih, weight_hh, bias_ih, bias
             st_A(i1)
             if single:
                 st_G1(batch_of[i0])
+                st_C1(batch_of[i0])
                 st_S2(batch_of[i0])
                 st_S1(i1)
                 st_G1(batch_of[i1])
+                st_C1(batch_of[i1])
                 st_G2(batch_of[i0])
                 st_S2(batch_of[i1])
                 st_G2(batch_of[i1])

@@ -21,22 +21,32 @@ GT = 2
 NG = NT // GT
 XC = 4
 XB = 4
-LEAD = 4
-MANUAL = True
-SMALL = ("g", "g", "v", "v")
-EB = 2
-TAILB = 2
+LEAD = 8
+SB_SET = (3,)
+SB_MOD = 4
+SMALL = ("g", "g", "g", "v")
 SMALL_TAIL = ("v", "v", "v", "v")
-SB_SET = (3, 5, 7)
-SB_MOD = 8
-QHEAD = 2
-TL = 5
-QL = 3
-D2 = 2
-D3 = 3
-HEADB = (1, 1, 1, 1)
+TAILB = 2
+EB = 2
 LINKB = 2
-CL = 2
+KH = 1
+KT = 13
+HEAD = [
+    [("H", 0), ("P", 1), ("P", 0), ("T", 1), ("T", 2), ("T", 0), ("P", 2), ("T", 3), ("P", 3), ("H", 1), ("T", 5), ("T", 4), ("P", 4), ("P", 5), ("T", 7), ("T", 6), ("M", 0), ("P", 6), ("T", 8), ("T", 10), ("P", 7), ("M", 1), ("P", 8), ("T", 9), ("T", 11), ("P", 9), ("M", 2), ("M", 3), ("P", 11), ("P", 10)],
+    [("B", 0), ("B", 1), ("W", 0), ("W", 3), ("W", 2), ("B", 2), ("Q", 0), ("B", 4), ("B", 5), ("A", 0), ("B", 6), ("Q", 1), ("A", 1), ("B", 8), ("B", 9), ("A", 2), ("A", 3), ("B", 10)],
+    [("HC", 0), ("W", 1), ("E", 1), ("E", 2), ("E", 0), ("E", 3), ("B", 3), ("HC", 1), ("E", 5), ("E", 4), ("E", 7), ("E", 6), ("B", 7), ("E", 10), ("E", 8), ("E", 9), ("E", 11), ("S1", 0), ("B", 11)],
+    [],
+]
+TAIL = [
+    [("T", 61), ("M", 52), ("P", 60), ("P", 61), ("T", 62), ("M", 53), ("T", 60), ("T", 63), ("M", 54), ("M", 55), ("M", 56), ("M", 57), ("M", 58), ("M", 59), ("P", 62), ("M", 60), ("M", 61), ("P", 63), ("M", 62), ("M", 63)],
+    [("G2", 10), ("Q", 14), ("A", 52), ("B", 60), ("A", 53), ("A", 54), ("B", 61), ("A", 55), ("G2", 11), ("Q", 15), ("A", 56), ("A", 57), ("A", 58), ("A", 59), ("G2", 12), ("A", 61), ("A", 60), ("B", 62), ("A", 62), ("A", 63), ("G1", 15), ("C1", 15), ("G2", 13), ("G1", 16), ("C1", 16), ("G2", 14), ("G2", 15), ("G2", 16)],
+    [("S1", 25), ("S2", 11), ("E", 61), ("E", 62), ("E", 60), ("E", 63), ("S1", 26), ("S1", 27), ("S2", 12), ("S1", 28), ("S1", 29), ("S2", 13), ("B", 63), ("S1", 30), ("S1", 31), ("S2", 14), ("S2", 15), ("S2", 16)],
+    [("G1", 12), ("C1", 12), ("G1", 13), ("C1", 13), ("G1", 14), ("C1", 14)],
+]
+PE_ORDER = [("H", 3, 0), ("M", 0, 0), ("M", 0, 1), ("P", 2, 0), ("T", 2, 1), ("T", 2, 0), ("P", 2, 1), ("T", 2, 2), ("T", 2, 3), ("M", 0, 2), ("M", 0, 3), ("P", 2, 2), ("P", 2, 3)]
+V_ORDER = [("G2", -3, 0), ("W", -2, 2), ("Q", 1, 0), ("A", 0, 0), ("A", 0, 1), ("B", 2, 0), ("B", 2, 1), ("A", 0, 2), ("W", -1, 3), ("B", 1, 3), ("A", 0, 3), ("B", 2, 2), ("W", -3, 0)]
+S_ORDER = [("S1", -1, 1), ("HC", 3, 0), ("S2", -2, 0), ("W", -2, 1), ("E", 2, 1), ("E", 2, 0), ("E", 2, 2), ("S1", 0, 0), ("E", 2, 3), ("B", 2, 3)]
+G_ORDER = [("G1", -1, 0), ("C1", -1, 0)]
 
 FLOPS = 2 * BATCH * K_IN * GATES + 2 * BATCH * HID * GATES
 
@@ -54,16 +64,15 @@ def tile_symlstmcell_t_kernel(tc, x, h0, c0, weight_ih, weight_hh, bias_ih, bias
         xpool = ctx.enter_context(tc.tile_pool(name="xpool", bufs=XB))
         gpool = ctx.enter_context(tc.tile_pool(name="gpool", bufs=2))
         qpool = ctx.enter_context(tc.tile_pool(name="qpool", bufs=3))
-        tpool = ctx.enter_context(tc.tile_pool(name="tpool", bufs=LEAD + 3))
+        tpool = ctx.enter_context(tc.tile_pool(name="tpool", bufs=LEAD))
         apool = ctx.enter_context(tc.tile_pool(name="apool", bufs=4))
         opool = ctx.enter_context(tc.tile_pool(name="opool", bufs=4))
         lpool = ctx.enter_context(tc.tile_pool(name="lpool", bufs=1))
-        ps_x = ctx.enter_context(tc.psum_pool(name="ps_x", bufs=3))
+        hpool = ctx.enter_context(tc.tile_pool(name="hpool", bufs=3))
+        ps_x = ctx.enter_context(tc.psum_pool(name="ps_x", bufs=4))
         ps_g = ctx.enter_context(tc.psum_pool(name="ps_g", bufs=2))
         ps_p = ctx.enter_context(tc.psum_pool(name="ps_p", bufs=2))
-        ps_h = ctx.enter_context(tc.psum_pool(name="ps_h", bufs=1))
-        if MANUAL:
-            ctx.enter_context(tc.manual_schedule())
+        ctx.enter_context(tc.manual_schedule())
 
         eng = {"v": nc.vector, "g": nc.gpsimd}
 
@@ -130,6 +139,10 @@ def tile_symlstmcell_t_kernel(tc, x, h0, c0, weight_ih, weight_hh, bias_ih, bias
         ppss = {}
         gpss = {}
         tmps = {}
+        acts = {}
+        c1os = {}
+        tcbs = {}
+        NQ = NT // 4
 
         batches = []
         j0 = 0
@@ -141,112 +154,92 @@ def tile_symlstmcell_t_kernel(tc, x, h0, c0, weight_ih, weight_hh, bias_ih, bias
         for bi, (bj, bn, be) in enumerate(batches):
             for j in range(bj, bj + bn):
                 batch_of[j] = bi
-        acts = {}
-        c1os = {}
+        n_full = len([b for b in batches if b[1] == EB])
 
         def on_scalar(t):
             return t % SB_MOD in SB_SET
 
         def st_H(b):
-            h0t = ps_h.tile([P, 8, HID], BF16, name="h0t")
+            h0t = ps_x.tile([P, 8, HID], BF16, name="xt")
             blk = part_of(h0_parts, 8 * b, 8)
             for i in range(8):
                 nc.tensor.transpose(h0t[:, i, :], blk[:, i, :], ident_b[:])
             h0ts[b] = h0t
 
         def st_HC(b):
-            ht = const.tile([P, 8, HID], BF16, name="hT%d" % b)
+            ht = hpool.tile([P, 8, HID], BF16, name="ht")
             nc.scalar.copy(out=ht[:], in_=h0ts[b][:])
             hT[b] = ht
 
-        def st_P(j):
-            for jj in range(GT):
-                t = GT * j + jj
-                pps = ps_p.tile([P, GATES], F32, name="pps")
-                sc = on_scalar(t)
-                nc.tensor.matmul(out=pps[:], lhsT=hT[t // 8][:, t % 8, :], rhs=whh[:], start=True, stop=not sc)
-                if sc:
-                    nc.tensor.matmul(out=pps[:], lhsT=ones[:], rhs=btile[:], start=False, stop=True)
-                ppss[t] = pps
+        def st_P(t):
+            pps = ps_p.tile([P, GATES], F32, name="pps")
+            sc = on_scalar(t)
+            nc.tensor.matmul(out=pps[:], lhsT=hT[t // 8][:, t % 8, :], rhs=whh[:], start=True, stop=not sc)
+            if sc:
+                nc.tensor.matmul(out=pps[:], lhsT=ones[:], rhs=btile[:], start=False, stop=True)
+            ppss[t] = pps
 
-        def st_BV(j):
-            tmp = tpool.tile([P, GT, GATES], F32, name="tmp")
-            tmps[j] = tmp
-            for jj in range(GT):
-                if not on_scalar(GT * j + jj):
-                    nc.vector.tensor_tensor(out=tmp[:, jj, :], in0=ppss[GT * j + jj][:], in1=bias_bc[:], op=ALU.add)
-
-        def st_BS(j):
-            for jj in range(GT):
-                if on_scalar(GT * j + jj):
-                    nc.scalar.copy(out=tmps[j][:, jj, :], in_=ppss[GT * j + jj][:])
-
-        def st_T(j):
-            for jj in range(GT):
-                t = GT * j + jj
-                xt = ps_x.tile([P, 4, P], F32, name="xt")
-                xw = xs[t // XC][:, t % XC, :].bitcast(F32)
-                for u in range(4):
-                    nc.tensor.transpose(xt[:, u, :], xw[:, P * u:P * (u + 1)], ident_f[:])
-                xts[t] = xt
-            if j % 2 == 1 and j // 2 + XB < NT // XC:
-                load_x(j // 2 + XB)
-
-        qb_of = {}
-        for j in range(NG):
-            if j < QHEAD:
-                qb_of[j] = (j, 1)
+        def st_B(t):
+            if t // GT not in tmps:
+                tmp = tpool.tile([P, GT, GATES], F32, name="tmp")
+                tmps[t // GT] = tmp
+            dst = tmps[t // GT][:, t % GT, :]
+            if on_scalar(t):
+                nc.scalar.copy(out=dst, in_=ppss[t][:])
             else:
-                qb_of[j] = (j - (j - QHEAD) % 2, 2)
+                nc.vector.tensor_tensor(out=dst, in0=ppss[t][:], in1=bias_bc[:], op=ALU.add)
 
-        def st_E(j):
-            f, n = qb_of[j]
-            if j == f:
-                grp = gpool.tile([P, n * GT, K_IN], BF16, name="grp", align_bytes=64)
-                grps[f] = grp
-            for jj in range(GT):
-                nc.scalar.copy(
-                    out=grps[f][:, (j - f) * GT + jj, :].bitcast(F32).rearrange("p (g b u) -> p g b u", g=2, u=2),
-                    in_=xts[GT * j + jj][:].rearrange("p (g u) b -> p g b u", u=2),
-                )
+        def st_T(t):
+            xt = ps_x.tile([P, 4, P], F32, name="xt")
+            xw = xs[t // XC][:, t % XC, :].bitcast(F32)
+            for u in range(4):
+                nc.tensor.transpose(xt[:, u, :], xw[:, P * u:P * (u + 1)], ident_f[:])
+            xts[t] = xt
+            if t % XC == XC - 1 and t // XC + XB < NT // XC:
+                load_x(t // XC + XB)
 
-        def st_Q(f):
-            n = qb_of[f][1]
-            cod = qpool.tile([P, n * GT * 256], U32, name="cod", align_bytes=64)
-            scl = qpool.tile([P, n * GT * 256], U8, name="scl", align_bytes=64)
-            nc.vector.quantize_mx(
-                out=cod[:].bitcast(FP8X4), scales=scl[:], in_=grps[f][:].rearrange("p j c -> p (j c)")
+        def st_E(t):
+            q = t // 4
+            if q not in grps:
+                grp = gpool.tile([P, 4, K_IN], BF16, name="grp", align_bytes=64)
+                grps[q] = grp
+            nc.scalar.copy(
+                out=grps[q][:, t % 4, :].bitcast(F32).rearrange("p (g b u) -> p g b u", g=2, u=2),
+                in_=xts[t][:].rearrange("p (g u) b -> p g b u", u=2),
             )
-            for j in range(f, f + n):
-                cods[j] = cod[:, (j - f) * GT * 256:(j - f + 1) * GT * 256]
-                scls[j] = scl[:, (j - f) * GT * 256:(j - f + 1) * GT * 256]
 
-        def st_M(j):
-            for jj in range(GT):
-                gps = ps_g.tile([P, GATES], F32, name="gps")
-                for g in range(2):
-                    lo = jj * 256 + g * P
-                    nc.tensor.matmul_mx(
-                        out=gps[:],
-                        lhsT=cods[j][:, lo:lo + P].bitcast(FP8X4),
-                        lhsT_scale=scls[j][:, lo:lo + P],
-                        rhs=wq[:, g, :].bitcast(FP8X4),
-                        rhs_scale=ws[:, g, :],
-                        start=(g == 0),
-                        stop=(g == 1),
-                    )
-                gpss[GT * j + jj] = gps
+        def st_Q(q):
+            cod = qpool.tile([P, 4 * 256], U32, name="cod", align_bytes=64)
+            scl = qpool.tile([P, 4 * 256], U8, name="scl", align_bytes=64)
+            nc.vector.quantize_mx(
+                out=cod[:].bitcast(FP8X4), scales=scl[:], in_=grps[q][:].rearrange("p j c -> p (j c)")
+            )
+            cods[q] = cod
+            scls[q] = scl
 
-        def st_A(j):
-            for jj in range(GT):
-                nc.vector.tensor_tensor(
-                    out=tmps[j][:, jj, :], in0=gpss[GT * j + jj][:], in1=tmps[j][:, jj, :], op=ALU.add
+        def st_M(t):
+            gps = ps_g.tile([P, GATES], F32, name="gps")
+            for g in range(2):
+                lo = (t % 4) * 256 + g * P
+                nc.tensor.matmul_mx(
+                    out=gps[:],
+                    lhsT=cods[t // 4][:, lo:lo + P].bitcast(FP8X4),
+                    lhsT_scale=scls[t // 4][:, lo:lo + P],
+                    rhs=wq[:, g, :].bitcast(FP8X4),
+                    rhs_scale=ws[:, g, :],
+                    start=(g == 0),
+                    stop=(g == 1),
                 )
+            gpss[t] = gps
+
+        def st_A(t):
+            dst = tmps[t // GT][:, t % GT, :]
+            nc.vector.tensor_tensor(out=dst, in0=gpss[t][:], in1=dst, op=ALU.add)
 
         def st_S1(j):
             bi = batch_of[j]
             bj, bn, be = batches[bi]
-            if j == bj:
+            if bi not in acts:
                 act = apool.tile([P, bn * GT, GATES], F32, name="act")
                 acts[bi] = act
             lo = (j - bj) * GT
@@ -254,21 +247,13 @@ def tile_symlstmcell_t_kernel(tc, x, h0, c0, weight_ih, weight_hh, bias_ih, bias
             nc.scalar.activation(out=act[:, :, HID:GATES], in_=tmps[j][:, :, HID:GATES], func=ACT.Sigmoid)
             nc.scalar.activation(out=act[:, :, 0:HID], in_=tmps[j][:, :, 0:HID], func=ACT.Tanh)
 
-        tcbs = {}
-
-        def link_tile(bn):
-            if bn == EB:
-                lk = lpool.tile([P, bn * GT, HID], F32, name="lk", bufs=LINKB)
-            else:
-                lk = lpool.tile([P, bn * GT, HID], F32, name="lkt", bufs=2)
-            return lk
-
         def st_G1(bi):
             bj, bn, be = batches[bi]
             act = acts[bi]
-            c1o = opool.tile([P, bn * GT, HID], F32, name="c1o")
-            c1os[bi] = c1o
-            m1 = link_tile(bn)
+            if bn == EB:
+                m1 = lpool.tile([P, bn * GT, HID], F32, name="lk", bufs=LINKB)
+            else:
+                m1 = lpool.tile([P, bn * GT, HID], F32, name="lkt", bufs=2)
             tcbs[bi] = m1
             eng[be[0]].tensor_tensor(out=m1[:], in0=act[:, :, 0:HID], in1=act[:, :, HID:2 * HID], op=ALU.mult)
             eng[be[1]].tensor_tensor(
@@ -278,145 +263,120 @@ def tile_symlstmcell_t_kernel(tc, x, h0, c0, weight_ih, weight_hh, bias_ih, bias
 
         def st_C1(bi):
             bj, bn, be = batches[bi]
-            c1o = c1os[bi]
+            c1o = opool.tile([P, bn * GT, HID], F32, name="c1o")
+            c1os[bi] = c1o
             eng[be[2]].tensor_tensor(out=c1o[:], in0=tcbs[bi][:], in1=acts[bi][:, :, 2 * HID:3 * HID], op=ALU.add)
             nc.sync.dma_start(out=c1v[:, GT * bj:GT * (bj + bn), :], in_=c1o[:])
 
         def st_S2(bi):
-            bj, bn, be = batches[bi]
             nc.scalar.activation(out=tcbs[bi][:], in_=c1os[bi][:], func=ACT.Tanh)
 
         def st_G2(bi):
             bj, bn, be = batches[bi]
-            act = acts[bi]
             h1o = opool.tile([P, bn * GT, HID], F32, name="h1o")
-            eng[be[3]].tensor_tensor(out=h1o[:], in0=tcbs[bi][:], in1=act[:, :, 3 * HID:GATES], op=ALU.mult)
+            eng[be[3]].tensor_tensor(out=h1o[:], in0=tcbs[bi][:], in1=acts[bi][:, :, 3 * HID:GATES], op=ALU.mult)
             nc.sync.dma_start(out=h1v[:, GT * bj:GT * (bj + bn), :], in_=h1o[:])
 
-        def plain(j):
-            st_P(j)
-            st_BV(j)
-            st_BS(j)
-
-        st_H(0)
-        st_HC(0)
         bps = ps_p.tile([P, GATES], F32, name="pps")
         nc.tensor.matmul(out=bps[:], lhsT=ones[:], rhs=btile[:], start=True, stop=True)
         bias_bc = const.tile([P, GATES], F32, name="bias_bc")
         nc.vector.tensor_copy(out=bias_bc[:], in_=bps[:])
-        st_H(1)
-        st_HC(1)
-        nb = 0
-        for j in range(HEADB[0]):
-            plain(nb)
-            nb += 1
-
         wview = w_raw[:].rearrange("p (g t c) -> p g t c", g=2, t=4)
         wq = const.tile([P, 2, GATES], U32, name="wq", align_bytes=64)
         ws = const.tile([P, 2, GATES], U8, name="ws", align_bytes=64)
         wg0 = const.tile([P, GATES, 4], BF16, name="wg0", align_bytes=64)
         wg1 = const.tile([P, GATES, 4], BF16, name="wg1", align_bytes=64)
-        nc.vector.tensor_copy(
-            out=wg0[:].rearrange("p (c i) t -> p c t i", i=4), in_=wview[:, 0].rearrange("p t (c i) -> p c t i", i=4)
-        )
-        nc.scalar.copy(
-            out=wg1[:].rearrange("p (c i) t -> p c t i", i=4), in_=wview[:, 1].rearrange("p t (c i) -> p c t i", i=4)
-        )
-        for j in range(HEADB[1]):
-            plain(nb)
-            nb += 1
-        nc.vector.quantize_mx(out=wq[:, 0, :].bitcast(FP8X4), scales=ws[:, 0, :], in_=wg0[:].rearrange("p c t -> p (c t)"))
-        nc.vector.quantize_mx(out=wq[:, 1, :].bitcast(FP8X4), scales=ws[:, 1, :], in_=wg1[:].rearrange("p c t -> p (c t)"))
-        st_T(0)
-        st_E(0)
-        st_T(1)
-        st_E(1)
-        for j in range(HEADB[2]):
-            plain(nb)
-            nb += 1
-        st_Q(0)
-        for j in range(HEADB[3]):
-            plain(nb)
-            nb += 1
-        st_Q(1)
-        assert nb <= LEAD
 
-        NK = NG // 2
-        assert nb == LEAD
+        def st_W(i):
+            if i == 0:
+                nc.vector.tensor_copy(
+                    out=wg0[:].rearrange("p (c i) t -> p c t i", i=4), in_=wview[:, 0].rearrange("p t (c i) -> p c t i", i=4)
+                )
+            elif i == 1:
+                nc.scalar.copy(
+                    out=wg1[:].rearrange("p (c i) t -> p c t i", i=4), in_=wview[:, 1].rearrange("p t (c i) -> p c t i", i=4)
+                )
+            elif i == 2:
+                nc.vector.quantize_mx(out=wq[:, 0, :].bitcast(FP8X4), scales=ws[:, 0, :], in_=wg0[:].rearrange("p c t -> p (c t)"))
+            else:
+                nc.vector.quantize_mx(out=wq[:, 1, :].bitcast(FP8X4), scales=ws[:, 1, :], in_=wg1[:].rearrange("p c t -> p (c t)"))
 
-        def plain_pe_v(j, first, count):
-            if j < NG:
-                st_P(j)
-                st_BV(j)
-
-        def maybe_H(j):
-            if j < NG and (j + 1) % 4 == 0 and j + 1 < NG and (j + 1) // 4 >= 2:
-                st_H((j + 1) // 4)
-                return [(j + 1) // 4]
+        def needs(s, i):
+            if s == "E":
+                return [("T", i)]
+            if s == "Q":
+                return [("E", 4 * i + r) for r in range(4)]
+            if s == "M":
+                return [("Q", i // 4), ("W", 2), ("W", 3)]
+            if s == "W":
+                return [("W", i - 2)] if i >= 2 else []
+            if s == "A":
+                return [("M", i), ("B", i)]
+            if s == "B":
+                return [("P", i)]
+            if s == "P":
+                return [("HC", i // 8)]
+            if s == "HC":
+                return [("H", i)]
+            if s == "S1":
+                return [("A", GT * i), ("A", GT * i + 1)]
+            if s == "G1":
+                bj, bn, be = batches[i]
+                old = [("G2", i - LINKB)] if (bn == EB and i >= LINKB) else []
+                return [("S1", j) for j in range(bj, bj + bn)] + old
+            if s == "C1":
+                return [("G1", i)]
+            if s == "S2":
+                return [("C1", i)]
+            if s == "G2":
+                return [("S2", i)]
             return []
 
-        n_full = len([b for b in batches if b[1] == EB])
-        for k in range(0, NK + 4):
-            i0 = 2 * k
-            i1 = 2 * k + 1
-            if 0 <= i0 - 1 < NG and batches[batch_of[i0 - 1]][1] == EB:
-                st_S1(i0 - 1)
-            if 2 <= k + 1 < NK:
-                st_Q(2 * (k + 1))
-            if 0 <= k - CL < n_full:
-                st_C1(k - CL)
-            if 0 <= k - 3 < n_full:
-                st_G2(k - 3)
-            if 0 <= k - 1 < n_full:
-                st_G1(k - 1)
-            if k >= NK:
-                if 0 <= k - 2 < n_full:
-                    st_S2(k - 2)
-                continue
-            g0 = i0 + LEAD
-            g1 = i1 + LEAD
-            st_M(i0)
-            st_A(i0)
-            if k == 0:
-                st_T(2)
-                st_E(2)
-            elif i0 + 4 < NG:
-                st_T(i0 + 4)
-                st_E(i0 + 4)
-            plain_pe_v(g0, 0, 2)
-            if g0 < NG:
-                st_BS(g0)
-            hs = maybe_H(g0)
-            single = batches[batch_of[i0]][1] == 1
-            if 0 <= k - 2 < n_full:
-                st_S2(k - 2)
-            st_S1(i0)
-            st_M(i1)
-            st_A(i1)
-            if single:
-                st_G1(batch_of[i0])
-                st_C1(batch_of[i0])
-                st_S2(batch_of[i0])
-                st_S1(i1)
-                st_G1(batch_of[i1])
-                st_C1(batch_of[i1])
-                st_G2(batch_of[i0])
-                st_S2(batch_of[i1])
-                st_G2(batch_of[i1])
-            if k == 0:
-                st_T(3)
-                st_E(3)
-                st_Q(2)
-                st_T(4)
-                st_E(4)
-                st_T(5)
-                st_E(5)
-            elif i1 + 4 < NG:
-                st_T(i1 + 4)
-                st_E(i1 + 4)
-            plain_pe_v(g1, 0, 2)
-            if g1 < NG:
-                st_BS(g1)
-            hs = hs + maybe_H(g1)
-            for hb in hs:
-                st_HC(hb)
+        count = {"T": NT, "E": NT, "Q": NQ, "M": NT, "A": NT, "B": NT, "P": NT, "H": NT // 8, "HC": NT // 8,
+                 "S1": NG, "G1": n_full, "C1": n_full, "S2": n_full, "G2": n_full, "W": 4}
+        per = {"T": 4, "E": 4, "Q": 1, "M": 4, "A": 4, "B": 4, "P": 4, "S1": 2, "G1": 1, "C1": 1, "S2": 1, "G2": 1}
+        run = {"T": st_T, "E": st_E, "Q": st_Q, "M": st_M, "A": st_A, "B": st_B, "P": st_P, "H": st_H, "HC": st_HC,
+               "S1": st_S1, "G1": st_G1, "C1": st_C1, "S2": st_S2, "G2": st_G2, "W": st_W}
+
+        def expand(order, mine):
+            out = []
+            for k in range(KH, KT):
+                for (s, ahead, r) in order:
+                    if s == "W":
+                        if k == ahead:
+                            out.append((s, r))
+                        continue
+                    if s == "H" or s == "HC":
+                        if (k + ahead) % 2 == r and 0 <= (k + ahead) // 2 < count[s]:
+                            out.append((s, (k + ahead) // 2))
+                        continue
+                    i = per[s] * (k + ahead) + r
+                    if 0 <= k + ahead and 0 <= i < count[s] and mine(s, i):
+                        if s == "S1" and batches[batch_of[i]][1] != EB:
+                            continue
+                        out.append((s, i))
+            return out
+
+        lists = [
+            HEAD[0] + expand(PE_ORDER, lambda s, i: True) + TAIL[0],
+            HEAD[1] + expand(V_ORDER, lambda s, i: s != "B" or not on_scalar(i)) + TAIL[1],
+            HEAD[2] + expand(S_ORDER, lambda s, i: s != "B" or on_scalar(i)) + TAIL[2],
+            HEAD[3] + expand(G_ORDER, lambda s, i: True) + TAIL[3],
+        ]
+
+        done = set()
+        pos = [0, 0, 0, 0]
+        left = sum([len(li) for li in lists])
+        while left > 0:
+            moved = False
+            for e in range(4):
+                while pos[e] < len(lists[e]):
+                    s, i = lists[e][pos[e]]
+                    if not all([d in done for d in needs(s, i)]):
+                        break
+                    run[s](i)
+                    done.add((s, i))
+                    pos[e] += 1
+                    left -= 1
+                    moved = True
+            assert moved, "the orders wait for each other"

@@ -15,87 +15,92 @@ P = 128
 BATCH = 8192
 K_IN = 1024
 HID = 128
-GATES = 512
+GATES = 4 * HID
+PASSES = K_IN // 512
 NT = BATCH // P
-GT = 2
-NG = NT // GT
-XC = 4
-XB = 4
-LEAD = 8
-SB_SET = (3,)
-SB_MOD = 4
-SMALL = ("g", "g", "g", "v")
-SMALL_TAIL = ("v", "v", "v", "v")
-TAILB = 2
-EB = 2
-LINKB = 2
-KH = 1
-KT = 13
-HEAD = [
-    [("H", 0), ("P", 1), ("P", 0), ("T", 1), ("T", 2), ("T", 0), ("P", 2), ("T", 3), ("P", 3), ("H", 1), ("T", 5), ("T", 4), ("P", 4), ("P", 5), ("T", 7), ("T", 6), ("M", 0), ("P", 6), ("T", 8), ("T", 10), ("P", 7), ("M", 1), ("P", 8), ("T", 9), ("T", 11), ("P", 9), ("M", 2), ("M", 3), ("P", 11), ("P", 10)],
-    [("B", 0), ("B", 1), ("W", 0), ("W", 3), ("W", 2), ("B", 2), ("Q", 0), ("B", 4), ("B", 5), ("A", 0), ("B", 6), ("Q", 1), ("A", 1), ("B", 8), ("B", 9), ("A", 2), ("A", 3), ("B", 10)],
-    [("HC", 0), ("W", 1), ("E", 1), ("E", 2), ("E", 0), ("E", 3), ("B", 3), ("HC", 1), ("E", 5), ("E", 4), ("E", 7), ("E", 6), ("B", 7), ("E", 10), ("E", 8), ("E", 9), ("E", 11), ("S1", 0), ("B", 11)],
-    [],
-]
-TAIL = [
-    [("T", 61), ("M", 52), ("P", 60), ("P", 61), ("T", 62), ("M", 53), ("T", 60), ("T", 63), ("M", 54), ("M", 55), ("M", 56), ("M", 57), ("M", 58), ("M", 59), ("P", 62), ("M", 60), ("M", 61), ("P", 63), ("M", 62), ("M", 63)],
-    [("G2", 10), ("Q", 14), ("A", 52), ("B", 60), ("A", 53), ("A", 54), ("B", 61), ("A", 55), ("G2", 11), ("Q", 15), ("A", 56), ("A", 57), ("A", 58), ("A", 59), ("G2", 12), ("A", 61), ("A", 60), ("B", 62), ("A", 62), ("A", 63), ("G1", 15), ("C1", 15), ("G2", 13), ("G1", 16), ("C1", 16), ("G2", 14), ("G2", 15), ("G2", 16)],
-    [("S1", 25), ("S2", 11), ("E", 61), ("E", 62), ("E", 60), ("E", 63), ("S1", 26), ("S1", 27), ("S2", 12), ("S1", 28), ("S1", 29), ("S2", 13), ("B", 63), ("S1", 30), ("S1", 31), ("S2", 14), ("S2", 15), ("S2", 16)],
-    [("G1", 12), ("C1", 12), ("G1", 13), ("C1", 13), ("G1", 14), ("C1", 14)],
-]
-PE_ORDER = [("H", 3, 0), ("M", 0, 0), ("M", 0, 1), ("P", 2, 0), ("T", 2, 1), ("T", 2, 0), ("P", 2, 1), ("T", 2, 2), ("T", 2, 3), ("M", 0, 2), ("M", 0, 3), ("P", 2, 2), ("P", 2, 3)]
-V_ORDER = [("G2", -3, 0), ("W", -2, 2), ("Q", 1, 0), ("A", 0, 0), ("A", 0, 1), ("B", 2, 0), ("B", 2, 1), ("A", 0, 2), ("W", -1, 3), ("B", 1, 3), ("A", 0, 3), ("B", 2, 2), ("W", -3, 0)]
-S_ORDER = [("S1", -1, 1), ("HC", 3, 0), ("S2", -2, 0), ("W", -2, 1), ("E", 2, 1), ("E", 2, 0), ("E", 2, 2), ("S1", 0, 0), ("E", 2, 3), ("B", 2, 3)]
-G_ORDER = [("G1", -1, 0), ("C1", -1, 0)]
+QUAD = 4
+NQ = NT // QUAD
+PAIR = 2
+H_BLOCK = 8
 
 FLOPS = 2 * BATCH * K_IN * GATES + 2 * BATCH * HID * GATES
+
+LAST_TILES = 4
+LAST_BATCHES = [(60, 2), (62, 1), (63, 1)]
+N_FULL = (NT - LAST_TILES) // QUAD
+
+X_BUFS = 4
+GROUPED_BUFS = 2
+CODES_BUFS = 2
+SUM_BUFS = 6
+ACT_BUFS = 4
+OUT_BUFS = 4
+LINK_BUFS = 2
+HT_BUFS = 3
+BANKS_T = 4
+BANKS_MX = 2
+BANKS_PLAIN = 2
+
+FIRST_PERIOD = -3
+TENSOR_ORDER = [
+    ("h_t", 3, 0), ("mx", 0, 0), ("mx", 0, 1), ("plain", 2, 0), ("x_t", 2, 0), ("x_t", 2, 1), ("plain", 2, 1),
+    ("x_t", 2, 2), ("x_t", 2, 3), ("mx", 0, 2), ("mx", 0, 3), ("plain", 2, 2), ("plain", 2, 3),
+]
+VECTOR_ORDER = [
+    ("h1", -3, 0), ("quant", 1, 0), ("add", 0, 0), ("add", 0, 1), ("plain_out", 2, 0), ("plain_out", 2, 1),
+    ("add", 0, 2), ("add", 0, 3), ("plain_out", 2, 2),
+]
+SCALAR_ORDER = [
+    ("gates", -1, 1), ("h_out", 3, 0), ("tanh_c", -2, 0), ("x_out", 2, 0), ("x_out", 2, 1), ("x_out", 2, 2),
+    ("gates", 0, 0), ("x_out", 2, 3), ("plain_out", 2, 3),
+]
+GPSIMD_ORDER = [("prod", -1, 0), ("c1", -1, 0)]
 
 
 def tile_symlstmcell_t_kernel(tc, x, h0, c0, weight_ih, weight_hh, bias_ih, bias_hh, out_0, out_1):
     nc = tc.nc
-    xv = x.rearrange("(p t) k -> p t k", t=NT)
-    h0v = h0.rearrange("(p t) k -> p t k", t=NT)
-    c0v = c0.rearrange("(p t) k -> p t k", t=NT)
-    h1v = out_0.rearrange("(p t) u -> p t u", t=NT)
-    c1v = out_1.rearrange("(p t) u -> p t u", t=NT)
+    x_view = x.rearrange("(p t) k -> p t k", t=NT)
+    h0_view = h0.rearrange("(p t) k -> p t k", t=NT)
+    c0_view = c0.rearrange("(p t) k -> p t k", t=NT)
+    h1_view = out_0.rearrange("(p t) u -> p t u", t=NT)
+    c1_view = out_1.rearrange("(p t) u -> p t u", t=NT)
 
     with ExitStack() as ctx:
         const = ctx.enter_context(tc.tile_pool(name="const", bufs=1))
-        xpool = ctx.enter_context(tc.tile_pool(name="xpool", bufs=XB))
-        gpool = ctx.enter_context(tc.tile_pool(name="gpool", bufs=2))
-        qpool = ctx.enter_context(tc.tile_pool(name="qpool", bufs=3))
-        tpool = ctx.enter_context(tc.tile_pool(name="tpool", bufs=LEAD))
-        apool = ctx.enter_context(tc.tile_pool(name="apool", bufs=4))
-        opool = ctx.enter_context(tc.tile_pool(name="opool", bufs=4))
-        lpool = ctx.enter_context(tc.tile_pool(name="lpool", bufs=1))
-        hpool = ctx.enter_context(tc.tile_pool(name="hpool", bufs=3))
-        ps_x = ctx.enter_context(tc.psum_pool(name="ps_x", bufs=4))
-        ps_g = ctx.enter_context(tc.psum_pool(name="ps_g", bufs=2))
-        ps_p = ctx.enter_context(tc.psum_pool(name="ps_p", bufs=2))
+        x_pool = ctx.enter_context(tc.tile_pool(name="x_pool", bufs=X_BUFS))
+        grouped_pool = ctx.enter_context(tc.tile_pool(name="grouped_pool", bufs=GROUPED_BUFS))
+        codes_pool = ctx.enter_context(tc.tile_pool(name="codes_pool", bufs=CODES_BUFS))
+        sum_pool = ctx.enter_context(tc.tile_pool(name="sum_pool", bufs=SUM_BUFS))
+        act_pool = ctx.enter_context(tc.tile_pool(name="act_pool", bufs=ACT_BUFS))
+        out_pool = ctx.enter_context(tc.tile_pool(name="out_pool", bufs=OUT_BUFS))
+        link_pool = ctx.enter_context(tc.tile_pool(name="link_pool", bufs=LINK_BUFS))
+        last_pool = ctx.enter_context(tc.tile_pool(name="last_pool", bufs=len(LAST_BATCHES)))
+        ht_pool = ctx.enter_context(tc.tile_pool(name="ht_pool", bufs=HT_BUFS))
+        banks_t = ctx.enter_context(tc.psum_pool(name="banks_t", bufs=BANKS_T))
+        banks_mx = ctx.enter_context(tc.psum_pool(name="banks_mx", bufs=BANKS_MX))
+        banks_plain = ctx.enter_context(tc.psum_pool(name="banks_plain", bufs=BANKS_PLAIN))
         ctx.enter_context(tc.manual_schedule())
 
-        eng = {"v": nc.vector, "g": nc.gpsimd}
-
-        ident_f = const.tile([P, P], F32, name="ident_f")
-        ident_b = const.tile([P, P], BF16, name="ident_b")
-        make_identity(nc, ident_b[:])
-        make_identity(nc, ident_f[:])
-        btile = const.tile([P, GATES], BF16, name="btile")
-        nc.vector.memset(btile[:], 0.0)
+        ident_f32 = const.tile([P, P], F32, name="ident_f32")
+        ident_bf16 = const.tile([P, P], BF16, name="ident_bf16")
+        make_identity(nc, ident_bf16[:])
+        make_identity(nc, ident_f32[:])
+        bias_rows = const.tile([P, GATES], BF16, name="bias_rows")
+        nc.vector.memset(bias_rows[:], 0.0)
         ones = const.tile([P, P], BF16, name="ones")
         nc.vector.memset(ones[:], 1.0)
         warm = const.tile([P, 1], F32, name="warm")
         nc.vector.memset(warm[:], 0.0)
-
-        nc.sync.dma_start(out=btile[0:1, :], in_=bias_ih.rearrange("(o n) -> o n", o=1))
-        nc.scalar.dma_start(out=btile[1:2, :], in_=bias_hh.rearrange("(o n) -> o n", o=1))
+        nc.sync.dma_start(out=bias_rows[0:1, :], in_=bias_ih.rearrange("(o n) -> o n", o=1))
+        nc.scalar.dma_start(out=bias_rows[1:2, :], in_=bias_hh.rearrange("(o n) -> o n", o=1))
         nc.scalar.activation(out=warm[:], in_=warm[:], func=ACT.Sigmoid)
 
         h0_parts = []
         c0_parts = []
+        x_tiles = {}
 
-        def load_part(parts, view, lo, hi, nm):
-            part = const.tile([P, hi - lo, HID], BF16, name="%s%d" % (nm, lo))
+        def load_part(parts, view, lo, hi, label):
+            part = const.tile([P, hi - lo, HID], BF16, name="%s%d" % (label, lo))
             nc.sync.dma_start(out=part[:], in_=view[:, lo:hi, :])
             parts.append((lo, hi, part))
 
@@ -105,278 +110,280 @@ def tile_symlstmcell_t_kernel(tc, x, h0, c0, weight_ih, weight_hh, bias_ih, bias
             a, part = found[0]
             return part[:, lo - a:lo - a + n, :]
 
-        xs = {}
+        def load_x(q):
+            x_sb = x_pool.tile([P, QUAD, K_IN], BF16, name="x_sb")
+            nc.sync.dma_start(out=x_sb[:], in_=x_view[:, QUAD * q:QUAD * (q + 1), :])
+            x_tiles[q] = x_sb
 
-        def load_x(c):
-            xc = xpool.tile([P, XC, K_IN], BF16, name="xc")
-            nc.sync.dma_start(out=xc[:], in_=xv[:, XC * c:XC * (c + 1), :])
-            xs[c] = xc
-
-        load_part(h0_parts, h0v, 0, 16, "h0p")
-        whh = const.tile([P, GATES], BF16, name="whh")
-        nc.sync.dma_start(out=whh[:], in_=weight_hh)
-        w_raw = const.tile([P, 4 * K_IN], BF16, name="w_raw")
+        w_raw = const.tile([P, PASSES * 4 * GATES], BF16, name="w_raw")
         nc.sync.dma_start(
-            out=w_raw[:].rearrange("p (a r) -> p a r", a=4),
-            in_=weight_ih.rearrange("(a q e) c -> q a (e c)", a=4, e=2),
+            out=w_raw[:].rearrange("p (a r) -> p a r", a=2 * PASSES),
+            in_=weight_ih.rearrange("(a q e) c -> q a (e c)", a=2 * PASSES, e=2),
         )
+        load_part(h0_parts, h0_view, 0, 8, "h0_")
+        w_hh = const.tile([P, GATES], BF16, name="w_hh")
+        nc.sync.dma_start(out=w_hh[:], in_=weight_hh)
         load_x(0)
+        load_part(h0_parts, h0_view, 8, 24, "h0_")
         load_x(1)
-        load_part(c0_parts, c0v, 0, 16, "c0p")
+        load_part(c0_parts, c0_view, 0, 16, "c0_")
         load_x(2)
-        load_part(h0_parts, h0v, 16, NT, "h0p")
+        load_part(h0_parts, h0_view, 24, NT, "h0_")
         load_x(3)
-        load_part(c0_parts, c0v, 16, NT, "c0p")
-        for c in range(4, XB):
-            load_x(c)
+        load_part(c0_parts, c0_view, 16, NT, "c0_")
 
-        hT = {}
-        h0ts = {}
-        xts = {}
-        grps = {}
-        cods = {}
-        scls = {}
-        ppss = {}
-        gpss = {}
-        tmps = {}
-        acts = {}
-        c1os = {}
-        tcbs = {}
-        NQ = NT // 4
-
-        batches = []
-        j0 = 0
-        while j0 < NG:
-            n = EB if j0 + EB <= NG - TAILB else 1
-            batches.append((j0, n, SMALL if n == EB else SMALL_TAIL))
-            j0 += n
-        batch_of = {}
-        for bi, (bj, bn, be) in enumerate(batches):
-            for j in range(bj, bj + bn):
-                batch_of[j] = bi
-        n_full = len([b for b in batches if b[1] == EB])
-
-        def on_scalar(t):
-            return t % SB_MOD in SB_SET
-
-        def st_H(b):
-            h0t = ps_x.tile([P, 8, HID], BF16, name="xt")
-            blk = part_of(h0_parts, 8 * b, 8)
-            for i in range(8):
-                nc.tensor.transpose(h0t[:, i, :], blk[:, i, :], ident_b[:])
-            h0ts[b] = h0t
-
-        def st_HC(b):
-            ht = hpool.tile([P, 8, HID], BF16, name="ht")
-            nc.scalar.copy(out=ht[:], in_=h0ts[b][:])
-            hT[b] = ht
-
-        def st_P(t):
-            pps = ps_p.tile([P, GATES], F32, name="pps")
-            sc = on_scalar(t)
-            nc.tensor.matmul(out=pps[:], lhsT=hT[t // 8][:, t % 8, :], rhs=whh[:], start=True, stop=not sc)
-            if sc:
-                nc.tensor.matmul(out=pps[:], lhsT=ones[:], rhs=btile[:], start=False, stop=True)
-            ppss[t] = pps
-
-        def st_B(t):
-            if t // GT not in tmps:
-                tmp = tpool.tile([P, GT, GATES], F32, name="tmp")
-                tmps[t // GT] = tmp
-            dst = tmps[t // GT][:, t % GT, :]
-            if on_scalar(t):
-                nc.scalar.copy(out=dst, in_=ppss[t][:])
-            else:
-                nc.vector.tensor_tensor(out=dst, in0=ppss[t][:], in1=bias_bc[:], op=ALU.add)
-
-        def st_T(t):
-            xt = ps_x.tile([P, 4, P], F32, name="xt")
-            xw = xs[t // XC][:, t % XC, :].bitcast(F32)
-            for u in range(4):
-                nc.tensor.transpose(xt[:, u, :], xw[:, P * u:P * (u + 1)], ident_f[:])
-            xts[t] = xt
-            if t % XC == XC - 1 and t // XC + XB < NT // XC:
-                load_x(t // XC + XB)
-
-        def st_E(t):
-            q = t // 4
-            if q not in grps:
-                grp = gpool.tile([P, 4, K_IN], BF16, name="grp", align_bytes=64)
-                grps[q] = grp
-            nc.scalar.copy(
-                out=grps[q][:, t % 4, :].bitcast(F32).rearrange("p (g b u) -> p g b u", g=2, u=2),
-                in_=xts[t][:].rearrange("p (g u) b -> p g b u", u=2),
-            )
-
-        def st_Q(q):
-            cod = qpool.tile([P, 4 * 256], U32, name="cod", align_bytes=64)
-            scl = qpool.tile([P, 4 * 256], U8, name="scl", align_bytes=64)
-            nc.vector.quantize_mx(
-                out=cod[:].bitcast(FP8X4), scales=scl[:], in_=grps[q][:].rearrange("p j c -> p (j c)")
-            )
-            cods[q] = cod
-            scls[q] = scl
-
-        def st_M(t):
-            gps = ps_g.tile([P, GATES], F32, name="gps")
-            for g in range(2):
-                lo = (t % 4) * 256 + g * P
-                nc.tensor.matmul_mx(
-                    out=gps[:],
-                    lhsT=cods[t // 4][:, lo:lo + P].bitcast(FP8X4),
-                    lhsT_scale=scls[t // 4][:, lo:lo + P],
-                    rhs=wq[:, g, :].bitcast(FP8X4),
-                    rhs_scale=ws[:, g, :],
-                    start=(g == 0),
-                    stop=(g == 1),
-                )
-            gpss[t] = gps
-
-        def st_A(t):
-            dst = tmps[t // GT][:, t % GT, :]
-            nc.vector.tensor_tensor(out=dst, in0=gpss[t][:], in1=dst, op=ALU.add)
-
-        def st_S1(j):
-            bi = batch_of[j]
-            bj, bn, be = batches[bi]
-            if bi not in acts:
-                act = apool.tile([P, bn * GT, GATES], F32, name="act")
-                acts[bi] = act
-            lo = (j - bj) * GT
-            act = acts[bi][:, lo:lo + GT, :]
-            nc.scalar.activation(out=act[:, :, HID:GATES], in_=tmps[j][:, :, HID:GATES], func=ACT.Sigmoid)
-            nc.scalar.activation(out=act[:, :, 0:HID], in_=tmps[j][:, :, 0:HID], func=ACT.Tanh)
-
-        def st_G1(bi):
-            bj, bn, be = batches[bi]
-            act = acts[bi]
-            if bn == EB:
-                m1 = lpool.tile([P, bn * GT, HID], F32, name="lk", bufs=LINKB)
-            else:
-                m1 = lpool.tile([P, bn * GT, HID], F32, name="lkt", bufs=2)
-            tcbs[bi] = m1
-            eng[be[0]].tensor_tensor(out=m1[:], in0=act[:, :, 0:HID], in1=act[:, :, HID:2 * HID], op=ALU.mult)
-            eng[be[1]].tensor_tensor(
-                out=act[:, :, 2 * HID:3 * HID], in0=act[:, :, 2 * HID:3 * HID],
-                in1=part_of(c0_parts, GT * bj, GT * bn), op=ALU.mult
-            )
-
-        def st_C1(bi):
-            bj, bn, be = batches[bi]
-            c1o = opool.tile([P, bn * GT, HID], F32, name="c1o")
-            c1os[bi] = c1o
-            eng[be[2]].tensor_tensor(out=c1o[:], in0=tcbs[bi][:], in1=acts[bi][:, :, 2 * HID:3 * HID], op=ALU.add)
-            nc.sync.dma_start(out=c1v[:, GT * bj:GT * (bj + bn), :], in_=c1o[:])
-
-        def st_S2(bi):
-            nc.scalar.activation(out=tcbs[bi][:], in_=c1os[bi][:], func=ACT.Tanh)
-
-        def st_G2(bi):
-            bj, bn, be = batches[bi]
-            h1o = opool.tile([P, bn * GT, HID], F32, name="h1o")
-            eng[be[3]].tensor_tensor(out=h1o[:], in0=tcbs[bi][:], in1=acts[bi][:, :, 3 * HID:GATES], op=ALU.mult)
-            nc.sync.dma_start(out=h1v[:, GT * bj:GT * (bj + bn), :], in_=h1o[:])
-
-        bps = ps_p.tile([P, GATES], F32, name="pps")
-        nc.tensor.matmul(out=bps[:], lhsT=ones[:], rhs=btile[:], start=True, stop=True)
-        bias_bc = const.tile([P, GATES], F32, name="bias_bc")
-        nc.vector.tensor_copy(out=bias_bc[:], in_=bps[:])
-        wview = w_raw[:].rearrange("p (g t c) -> p g t c", g=2, t=4)
-        wq = const.tile([P, 2, GATES], U32, name="wq", align_bytes=64)
-        ws = const.tile([P, 2, GATES], U8, name="ws", align_bytes=64)
-        wg0 = const.tile([P, GATES, 4], BF16, name="wg0", align_bytes=64)
-        wg1 = const.tile([P, GATES, 4], BF16, name="wg1", align_bytes=64)
-
-        def st_W(i):
-            if i == 0:
-                nc.vector.tensor_copy(
-                    out=wg0[:].rearrange("p (c i) t -> p c t i", i=4), in_=wview[:, 0].rearrange("p t (c i) -> p c t i", i=4)
-                )
-            elif i == 1:
-                nc.scalar.copy(
-                    out=wg1[:].rearrange("p (c i) t -> p c t i", i=4), in_=wview[:, 1].rearrange("p t (c i) -> p c t i", i=4)
-                )
-            elif i == 2:
-                nc.vector.quantize_mx(out=wq[:, 0, :].bitcast(FP8X4), scales=ws[:, 0, :], in_=wg0[:].rearrange("p c t -> p (c t)"))
-            else:
-                nc.vector.quantize_mx(out=wq[:, 1, :].bitcast(FP8X4), scales=ws[:, 1, :], in_=wg1[:].rearrange("p c t -> p (c t)"))
-
-        def needs(s, i):
-            if s == "E":
-                return [("T", i)]
-            if s == "Q":
-                return [("E", 4 * i + r) for r in range(4)]
-            if s == "M":
-                return [("Q", i // 4), ("W", 2), ("W", 3)]
-            if s == "W":
-                return [("W", i - 2)] if i >= 2 else []
-            if s == "A":
-                return [("M", i), ("B", i)]
-            if s == "B":
-                return [("P", i)]
-            if s == "P":
-                return [("HC", i // 8)]
-            if s == "HC":
-                return [("H", i)]
-            if s == "S1":
-                return [("A", GT * i), ("A", GT * i + 1)]
-            if s == "G1":
-                bj, bn, be = batches[i]
-                old = [("G2", i - LINKB)] if (bn == EB and i >= LINKB) else []
-                return [("S1", j) for j in range(bj, bj + bn)] + old
-            if s == "C1":
-                return [("G1", i)]
-            if s == "S2":
-                return [("C1", i)]
-            if s == "G2":
-                return [("S2", i)]
-            return []
-
-        count = {"T": NT, "E": NT, "Q": NQ, "M": NT, "A": NT, "B": NT, "P": NT, "H": NT // 8, "HC": NT // 8,
-                 "S1": NG, "G1": n_full, "C1": n_full, "S2": n_full, "G2": n_full, "W": 4}
-        per = {"T": 4, "E": 4, "Q": 1, "M": 4, "A": 4, "B": 4, "P": 4, "S1": 2, "G1": 1, "C1": 1, "S2": 1, "G2": 1}
-        run = {"T": st_T, "E": st_E, "Q": st_Q, "M": st_M, "A": st_A, "B": st_B, "P": st_P, "H": st_H, "HC": st_HC,
-               "S1": st_S1, "G1": st_G1, "C1": st_C1, "S2": st_S2, "G2": st_G2, "W": st_W}
-
-        def expand(order, mine):
-            out = []
-            for k in range(KH, KT):
-                for (s, ahead, r) in order:
-                    if s == "W":
-                        if k == ahead:
-                            out.append((s, r))
-                        continue
-                    if s == "H" or s == "HC":
-                        if (k + ahead) % 2 == r and 0 <= (k + ahead) // 2 < count[s]:
-                            out.append((s, (k + ahead) // 2))
-                        continue
-                    i = per[s] * (k + ahead) + r
-                    if 0 <= k + ahead and 0 <= i < count[s] and mine(s, i):
-                        if s == "S1" and batches[batch_of[i]][1] != EB:
-                            continue
-                        out.append((s, i))
-            return out
-
-        lists = [
-            HEAD[0] + expand(PE_ORDER, lambda s, i: True) + TAIL[0],
-            HEAD[1] + expand(V_ORDER, lambda s, i: s != "B" or not on_scalar(i)) + TAIL[1],
-            HEAD[2] + expand(S_ORDER, lambda s, i: s != "B" or on_scalar(i)) + TAIL[2],
-            HEAD[3] + expand(G_ORDER, lambda s, i: True) + TAIL[3],
+        bias_bank = banks_plain.tile([P, GATES], F32, name="plain_bank")
+        nc.tensor.matmul(out=bias_bank[:], lhsT=ones[:], rhs=bias_rows[:], start=True, stop=True)
+        bias_all = const.tile([P, GATES], F32, name="bias_all")
+        nc.scalar.copy(out=bias_all[:], in_=bias_bank[:])
+        w_view = w_raw[:].rearrange("p (g t c) -> p g t c", g=PASSES, t=4)
+        w_codes = const.tile([P, PASSES, GATES], U32, name="w_codes", align_bytes=64)
+        w_scales = const.tile([P, PASSES, GATES], U8, name="w_scales", align_bytes=64)
+        w_grouped = [
+            const.tile([P, GATES, 4], BF16, name="w_grouped%d" % g, align_bytes=64) for g in range(PASSES)
         ]
 
-        done = set()
-        pos = [0, 0, 0, 0]
-        left = sum([len(li) for li in lists])
+        units = [(PAIR * j, PAIR) for j in range(N_FULL * QUAD // PAIR)] + LAST_BATCHES
+        batches = [(QUAD * b, QUAD, nc.gpsimd) for b in range(N_FULL)] + [(lo, n, nc.vector) for (lo, n) in LAST_BATCHES]
+        n_pairs = N_FULL * QUAD // PAIR
+
+        def batch_of(u):
+            return u * PAIR // QUAD if u < n_pairs else N_FULL + u - n_pairs
+
+        def on_scalar(t):
+            return t % QUAD == QUAD - 1
+
+        h_banks = {}
+        h_t_tiles = {}
+        x_banks = {}
+        grouped = {}
+        codes = {}
+        scales = {}
+        plain_banks = {}
+        mx_banks = {}
+        sums = {}
+        acts = {}
+        links = {}
+        c1_tiles = {}
+
+        def w_group(g):
+            nc.vector.tensor_copy(
+                out=w_grouped[g][:].rearrange("p (c i) t -> p c t i", i=4),
+                in_=w_view[:, g].rearrange("p t (c i) -> p c t i", i=4),
+            )
+
+        def w_quant(g):
+            nc.vector.quantize_mx(
+                out=w_codes[:, g, :].bitcast(FP8X4),
+                scales=w_scales[:, g, :],
+                in_=w_grouped[g][:].rearrange("p c t -> p (c t)"),
+            )
+
+        def h_t(b):
+            bank = banks_t.tile([P, H_BLOCK, HID], BF16, name="t_bank")
+            block = part_of(h0_parts, H_BLOCK * b, H_BLOCK)
+            for i in range(H_BLOCK):
+                nc.tensor.transpose(bank[:, i, :], block[:, i, :], ident_bf16[:])
+            h_banks[b] = bank
+
+        def h_out(b):
+            h_t_sb = ht_pool.tile([P, H_BLOCK, HID], BF16, name="h_t_sb")
+            nc.scalar.copy(out=h_t_sb[:], in_=h_banks[b][:])
+            h_t_tiles[b] = h_t_sb
+
+        def plain(t):
+            bank = banks_plain.tile([P, GATES], F32, name="plain_bank")
+            with_bias = on_scalar(t)
+            nc.tensor.matmul(
+                out=bank[:], lhsT=h_t_tiles[t // H_BLOCK][:, t % H_BLOCK, :], rhs=w_hh[:], start=True, stop=not with_bias
+            )
+            if with_bias:
+                nc.tensor.matmul(out=bank[:], lhsT=ones[:], rhs=bias_rows[:], start=False, stop=True)
+            plain_banks[t] = bank
+
+        def plain_out(t):
+            if t // PAIR not in sums:
+                gate_sum = sum_pool.tile([P, PAIR, GATES], F32, name="gate_sum")
+                sums[t // PAIR] = gate_sum
+            dst = sums[t // PAIR][:, t % PAIR, :]
+            if on_scalar(t):
+                nc.scalar.copy(out=dst, in_=plain_banks[t][:])
+            else:
+                nc.vector.tensor_tensor(out=dst, in0=plain_banks[t][:], in1=bias_all[:], op=ALU.add)
+
+        def x_t(t):
+            bank = banks_t.tile([P, 2 * PASSES, P], F32, name="t_bank")
+            words = x_tiles[t // QUAD][:, t % QUAD, :].bitcast(F32)
+            for a in range(2 * PASSES):
+                nc.tensor.transpose(bank[:, a, :], words[:, P * a:P * (a + 1)], ident_f32[:])
+            x_banks[t] = bank
+            if t % QUAD == QUAD - 1 and t // QUAD + X_BUFS < NQ:
+                load_x(t // QUAD + X_BUFS)
+
+        def x_out(t):
+            q = t // QUAD
+            if q not in grouped:
+                x_grouped = grouped_pool.tile([P, QUAD, K_IN], BF16, name="x_grouped", align_bytes=64)
+                grouped[q] = x_grouped
+            nc.scalar.copy(
+                out=grouped[q][:, t % QUAD, :].bitcast(F32).rearrange("p (g b u) -> p g b u", g=PASSES, u=2),
+                in_=x_banks[t][:].rearrange("p (g u) b -> p g b u", u=2),
+            )
+
+        def quant(q):
+            x_codes = codes_pool.tile([P, QUAD * PASSES * P], U32, name="x_codes", align_bytes=64)
+            x_scales = codes_pool.tile([P, QUAD * PASSES * P], U8, name="x_scales", align_bytes=64)
+            nc.vector.quantize_mx(
+                out=x_codes[:].bitcast(FP8X4), scales=x_scales[:], in_=grouped[q][:].rearrange("p j c -> p (j c)")
+            )
+            codes[q] = x_codes
+            scales[q] = x_scales
+
+        def mx(t):
+            bank = banks_mx.tile([P, GATES], F32, name="mx_bank")
+            for g in range(PASSES):
+                lo = ((t % QUAD) * PASSES + g) * P
+                nc.tensor.matmul_mx(
+                    out=bank[:],
+                    lhsT=codes[t // QUAD][:, lo:lo + P].bitcast(FP8X4),
+                    lhsT_scale=scales[t // QUAD][:, lo:lo + P],
+                    rhs=w_codes[:, g, :].bitcast(FP8X4),
+                    rhs_scale=w_scales[:, g, :],
+                    start=(g == 0),
+                    stop=(g == PASSES - 1),
+                )
+            mx_banks[t] = bank
+
+        def add(t):
+            dst = sums[t // PAIR][:, t % PAIR, :]
+            nc.vector.tensor_tensor(out=dst, in0=mx_banks[t][:], in1=dst, op=ALU.add)
+
+        def gates(u):
+            b = batch_of(u)
+            b_lo, b_n, engine = batches[b]
+            u_lo, u_n = units[u]
+            if b not in acts:
+                act = act_pool.tile([P, b_n, GATES], F32, name="act")
+                acts[b] = act
+            dst = acts[b][:, u_lo - b_lo:u_lo - b_lo + u_n, :]
+            src = sums[u_lo // PAIR][:, u_lo % PAIR:u_lo % PAIR + u_n, :]
+            nc.scalar.activation(out=dst[:, :, HID:GATES], in_=src[:, :, HID:GATES], func=ACT.Sigmoid)
+            nc.scalar.activation(out=dst[:, :, 0:HID], in_=src[:, :, 0:HID], func=ACT.Tanh)
+
+        def prod(b):
+            b_lo, b_n, engine = batches[b]
+            act = acts[b]
+            if b < N_FULL:
+                link = link_pool.tile([P, b_n, HID], F32, name="link")
+            else:
+                link = last_pool.tile([P, b_n, HID], F32, name="last_link")
+            links[b] = link
+            engine.tensor_tensor(out=link[:], in0=act[:, :, 0:HID], in1=act[:, :, HID:2 * HID], op=ALU.mult)
+            engine.tensor_tensor(
+                out=act[:, :, 2 * HID:3 * HID], in0=act[:, :, 2 * HID:3 * HID], in1=part_of(c0_parts, b_lo, b_n), op=ALU.mult
+            )
+
+        def c1(b):
+            b_lo, b_n, engine = batches[b]
+            c1_sb = out_pool.tile([P, b_n, HID], F32, name="c1_sb")
+            c1_tiles[b] = c1_sb
+            engine.tensor_tensor(out=c1_sb[:], in0=links[b][:], in1=acts[b][:, :, 2 * HID:3 * HID], op=ALU.add)
+            nc.sync.dma_start(out=c1_view[:, b_lo:b_lo + b_n, :], in_=c1_sb[:])
+
+        def tanh_c(b):
+            nc.scalar.activation(out=links[b][:], in_=c1_tiles[b][:], func=ACT.Tanh)
+
+        def h1(b):
+            b_lo, b_n, engine = batches[b]
+            h1_sb = out_pool.tile([P, b_n, HID], F32, name="h1_sb")
+            nc.vector.tensor_tensor(out=h1_sb[:], in0=links[b][:], in1=acts[b][:, :, 3 * HID:GATES], op=ALU.mult)
+            nc.sync.dma_start(out=h1_view[:, b_lo:b_lo + b_n, :], in_=h1_sb[:])
+
+        run = {
+            "w_group": w_group, "w_quant": w_quant, "h_t": h_t, "h_out": h_out, "plain": plain, "plain_out": plain_out,
+            "x_t": x_t, "x_out": x_out, "quant": quant, "mx": mx, "add": add, "gates": gates, "prod": prod, "c1": c1,
+            "tanh_c": tanh_c, "h1": h1,
+        }
+        count = {
+            "x_t": NT, "x_out": NT, "quant": NQ, "mx": NT, "add": NT, "plain": NT, "plain_out": NT,
+            "h_t": NT // H_BLOCK, "h_out": NT // H_BLOCK, "gates": n_pairs,
+            "prod": N_FULL, "c1": N_FULL, "tanh_c": N_FULL, "h1": N_FULL,
+        }
+        per_period = {
+            "x_t": QUAD, "x_out": QUAD, "quant": 1, "mx": QUAD, "add": QUAD, "plain": QUAD, "plain_out": QUAD,
+            "gates": QUAD // PAIR, "prod": 1, "c1": 1, "tanh_c": 1, "h1": 1,
+        }
+
+        def needs(stage, i):
+            if stage == "w_quant":
+                return [("w_group", i)]
+            if stage == "x_out":
+                return [("x_t", i)]
+            if stage == "quant":
+                return [("x_out", QUAD * i + r) for r in range(QUAD)]
+            if stage == "mx":
+                return [("quant", i // QUAD)] + [("w_quant", g) for g in range(PASSES)]
+            if stage == "add":
+                return [("mx", i), ("plain_out", i)]
+            if stage == "plain_out":
+                return [("plain", i)] + ([("plain_out", i - 1)] if i > 0 else [])
+            if stage == "plain":
+                return [("h_out", i // H_BLOCK)]
+            if stage == "h_out":
+                return [("h_t", i)]
+            if stage == "gates":
+                return [("add", t) for t in range(units[i][0], units[i][0] + units[i][1])]
+            if stage == "prod":
+                frees_slot = [("h1", i - LINK_BUFS)] if LINK_BUFS <= i < N_FULL else []
+                return [("gates", u) for u in range(len(units)) if batch_of(u) == i] + frees_slot
+            if stage == "c1":
+                return [("prod", i)]
+            if stage == "tanh_c":
+                return [("c1", i)]
+            if stage == "h1":
+                return [("tanh_c", i)]
+            return []
+
+        def expand(order, mine):
+            items = []
+            for k in range(FIRST_PERIOD, NQ):
+                for (stage, ahead, r) in order:
+                    if stage == "h_t" or stage == "h_out":
+                        if (k + ahead) % 2 == r and 0 <= (k + ahead) // 2 < count[stage]:
+                            items.append((stage, (k + ahead) // 2))
+                        continue
+                    i = per_period[stage] * (k + ahead) + r
+                    if 0 <= k + ahead and i < count[stage] and mine(stage, i):
+                        items.append((stage, i))
+            return items
+
+        weight_first = [("w_group", g) for g in range(PASSES)] + [("w_quant", g) for g in range(PASSES)]
+        small = list(range(N_FULL, len(batches)))
+        vector_end = [("h1", N_FULL - 2)]
+        for b in small:
+            vector_end.extend([("prod", b), ("c1", b)])
+        vector_end.extend([("h1", b) for b in [N_FULL - 1] + small])
+        scalar_end = [("gates", n_pairs + j) for j in range(len(small))] + [("tanh_c", b) for b in [N_FULL - 1] + small]
+        orders = [
+            expand(TENSOR_ORDER, lambda stage, i: True),
+            weight_first + expand(VECTOR_ORDER, lambda stage, i: stage != "plain_out" or not on_scalar(i)) + vector_end,
+            expand(SCALAR_ORDER, lambda stage, i: stage != "plain_out" or on_scalar(i)) + scalar_end,
+            expand(GPSIMD_ORDER, lambda stage, i: True),
+        ]
+
+        written = set()
+        position = [0, 0, 0, 0]
+        left = sum([len(order) for order in orders])
         while left > 0:
             moved = False
-            for e in range(4):
-                while pos[e] < len(lists[e]):
-                    s, i = lists[e][pos[e]]
-                    if not all([d in done for d in needs(s, i)]):
+            for e in range(len(orders)):
+                while position[e] < len(orders[e]):
+                    stage, i = orders[e][position[e]]
+                    if not all([item in written for item in needs(stage, i)]):
                         break
-                    run[s](i)
-                    done.add((s, i))
-                    pos[e] += 1
+                    run[stage](i)
+                    written.add((stage, i))
+                    position[e] += 1
                     left -= 1
                     moved = True
-            assert moved, "the orders wait for each other"
+            assert moved, "the four orders wait for each other"

@@ -26,7 +26,7 @@ H_BLOCK = 8
 FLOPS = 2 * BATCH * K_IN * GATES + 2 * BATCH * HID * GATES
 
 LAST_TILES = 4
-LAST_BATCHES = [(60, 2), (62, 1), (63, 1)]
+LAST_BATCHES = [(NT - 4, 2), (NT - 2, 1), (NT - 1, 1)]
 N_FULL = (NT - LAST_TILES) // QUAD
 
 X_BUFS = 4
@@ -42,19 +42,6 @@ BANKS_MX = 2
 BANKS_PLAIN = 2
 
 FIRST_PERIOD = -3
-TENSOR_ORDER = [
-    ("h_t", 3, 0), ("mx", 0, 0), ("mx", 0, 1), ("plain", 2, 0), ("x_t", 2, 0), ("x_t", 2, 1), ("plain", 2, 1),
-    ("x_t", 2, 2), ("x_t", 2, 3), ("mx", 0, 2), ("mx", 0, 3), ("plain", 2, 2), ("plain", 2, 3),
-]
-VECTOR_ORDER = [
-    ("h1", -3, 0), ("quant", 1, 0), ("add", 0, 0), ("add", 0, 1), ("plain_out", 2, 0), ("plain_out", 2, 1),
-    ("add", 0, 2), ("add", 0, 3), ("plain_out", 2, 2),
-]
-SCALAR_ORDER = [
-    ("gates", -1, 1), ("h_out", 3, 0), ("tanh_c", -2, 0), ("x_out", 2, 0), ("x_out", 2, 1), ("x_out", 2, 2),
-    ("gates", 0, 0), ("x_out", 2, 3), ("plain_out", 2, 3),
-]
-GPSIMD_ORDER = [("prod", -1, 0), ("c1", -1, 0)]
 
 
 def tile_symlstmcell_t_kernel(tc, x, h0, c0, weight_ih, weight_hh, bias_ih, bias_hh, out_0, out_1):
@@ -105,10 +92,10 @@ def tile_symlstmcell_t_kernel(tc, x, h0, c0, weight_ih, weight_hh, bias_ih, bias
             parts.append((lo, hi, part))
 
         def part_of(parts, lo, n):
-            found = [(a, part) for (a, b, part) in parts if a <= lo and lo + n <= b]
+            found = [(first, part) for (first, end, part) in parts if first <= lo and lo + n <= end]
             assert len(found) == 1
-            a, part = found[0]
-            return part[:, lo - a:lo - a + n, :]
+            first, part = found[0]
+            return part[:, lo - first:lo - first + n, :]
 
         def load_x(q):
             x_sb = x_pool.tile([P, QUAD, K_IN], BF16, name="x_sb")
@@ -117,8 +104,8 @@ def tile_symlstmcell_t_kernel(tc, x, h0, c0, weight_ih, weight_hh, bias_ih, bias
 
         w_raw = const.tile([P, PASSES * 4 * GATES], BF16, name="w_raw")
         nc.sync.dma_start(
-            out=w_raw[:].rearrange("p (a r) -> p a r", a=2 * PASSES),
-            in_=weight_ih.rearrange("(a q e) c -> q a (e c)", a=2 * PASSES, e=2),
+            out=w_raw[:].rearrange("p (a n) -> p a n", a=2 * PASSES),
+            in_=weight_ih.rearrange("(a p e) c -> p a (e c)", a=2 * PASSES, e=2),
         )
         load_part(h0_parts, h0_view, 0, 8, "h0_")
         w_hh = const.tile([P, GATES], BF16, name="w_hh")
@@ -136,19 +123,19 @@ def tile_symlstmcell_t_kernel(tc, x, h0, c0, weight_ih, weight_hh, bias_ih, bias
         nc.tensor.matmul(out=bias_bank[:], lhsT=ones[:], rhs=bias_rows[:], start=True, stop=True)
         bias_all = const.tile([P, GATES], F32, name="bias_all")
         nc.scalar.copy(out=bias_all[:], in_=bias_bank[:])
-        w_view = w_raw[:].rearrange("p (g t c) -> p g t c", g=PASSES, t=4)
+        w_view = w_raw[:].rearrange("p (m v c) -> p m v c", m=PASSES, v=4)
         w_codes = const.tile([P, PASSES, GATES], U32, name="w_codes", align_bytes=64)
         w_scales = const.tile([P, PASSES, GATES], U8, name="w_scales", align_bytes=64)
         w_grouped = [
-            const.tile([P, GATES, 4], BF16, name="w_grouped%d" % g, align_bytes=64) for g in range(PASSES)
+            const.tile([P, GATES, 4], BF16, name="w_grouped%d" % m, align_bytes=64) for m in range(PASSES)
         ]
 
         units = [(PAIR * j, PAIR) for j in range(N_FULL * QUAD // PAIR)] + LAST_BATCHES
         batches = [(QUAD * b, QUAD, nc.gpsimd) for b in range(N_FULL)] + [(lo, n, nc.vector) for (lo, n) in LAST_BATCHES]
         n_pairs = N_FULL * QUAD // PAIR
 
-        def batch_of(u):
-            return u * PAIR // QUAD if u < n_pairs else N_FULL + u - n_pairs
+        def batch_of(unit):
+            return unit * PAIR // QUAD if unit < n_pairs else N_FULL + unit - n_pairs
 
         def on_scalar(t):
             return t % QUAD == QUAD - 1
@@ -166,32 +153,38 @@ def tile_symlstmcell_t_kernel(tc, x, h0, c0, weight_ih, weight_hh, bias_ih, bias
         links = {}
         c1_tiles = {}
 
-        def w_group(g):
+        def w_group(m):
             nc.vector.tensor_copy(
-                out=w_grouped[g][:].rearrange("p (c i) t -> p c t i", i=4),
-                in_=w_view[:, g].rearrange("p t (c i) -> p c t i", i=4),
+                out=w_grouped[m][:].rearrange("p (c i) v -> p c v i", i=4),
+                in_=w_view[:, m].rearrange("p v (c i) -> p c v i", i=4),
             )
 
-        def w_quant(g):
+        def w_quant(m):
             nc.vector.quantize_mx(
-                out=w_codes[:, g, :].bitcast(FP8X4),
-                scales=w_scales[:, g, :],
-                in_=w_grouped[g][:].rearrange("p c t -> p (c t)"),
+                out=w_codes[:, m, :].bitcast(FP8X4),
+                scales=w_scales[:, m, :],
+                in_=w_grouped[m][:].rearrange("p c v -> p (c v)"),
             )
 
         def h_t(b):
+            if not 0 <= b < NT // H_BLOCK:
+                return
             bank = banks_t.tile([P, H_BLOCK, HID], BF16, name="t_bank")
             block = part_of(h0_parts, H_BLOCK * b, H_BLOCK)
-            for i in range(H_BLOCK):
-                nc.tensor.transpose(bank[:, i, :], block[:, i, :], ident_bf16[:])
+            for j in range(H_BLOCK):
+                nc.tensor.transpose(bank[:, j, :], block[:, j, :], ident_bf16[:])
             h_banks[b] = bank
 
         def h_out(b):
+            if not 0 <= b < NT // H_BLOCK:
+                return
             h_t_sb = ht_pool.tile([P, H_BLOCK, HID], BF16, name="h_t_sb")
             nc.scalar.copy(out=h_t_sb[:], in_=h_banks[b][:])
             h_t_tiles[b] = h_t_sb
 
         def plain(t):
+            if not 0 <= t < NT:
+                return
             bank = banks_plain.tile([P, GATES], F32, name="plain_bank")
             with_bias = on_scalar(t)
             nc.tensor.matmul(
@@ -202,6 +195,8 @@ def tile_symlstmcell_t_kernel(tc, x, h0, c0, weight_ih, weight_hh, bias_ih, bias
             plain_banks[t] = bank
 
         def plain_out(t):
+            if not 0 <= t < NT:
+                return
             if t // PAIR not in sums:
                 gate_sum = sum_pool.tile([P, PAIR, GATES], F32, name="gate_sum")
                 sums[t // PAIR] = gate_sum
@@ -212,6 +207,8 @@ def tile_symlstmcell_t_kernel(tc, x, h0, c0, weight_ih, weight_hh, bias_ih, bias
                 nc.vector.tensor_tensor(out=dst, in0=plain_banks[t][:], in1=bias_all[:], op=ALU.add)
 
         def x_t(t):
+            if not 0 <= t < NT:
+                return
             bank = banks_t.tile([P, 2 * PASSES, P], F32, name="t_bank")
             words = x_tiles[t // QUAD][:, t % QUAD, :].bitcast(F32)
             for a in range(2 * PASSES):
@@ -221,56 +218,68 @@ def tile_symlstmcell_t_kernel(tc, x, h0, c0, weight_ih, weight_hh, bias_ih, bias
                 load_x(t // QUAD + X_BUFS)
 
         def x_out(t):
+            if not 0 <= t < NT:
+                return
             q = t // QUAD
             if q not in grouped:
                 x_grouped = grouped_pool.tile([P, QUAD, K_IN], BF16, name="x_grouped", align_bytes=64)
                 grouped[q] = x_grouped
             nc.scalar.copy(
-                out=grouped[q][:, t % QUAD, :].bitcast(F32).rearrange("p (g b u) -> p g b u", g=PASSES, u=2),
-                in_=x_banks[t][:].rearrange("p (g u) b -> p g b u", u=2),
+                out=grouped[q][:, t % QUAD, :].bitcast(F32).rearrange("p (m r u) -> p m r u", m=PASSES, u=2),
+                in_=x_banks[t][:].rearrange("p (m u) r -> p m r u", u=2),
             )
 
         def quant(q):
+            if not 0 <= q < NQ:
+                return
             x_codes = codes_pool.tile([P, QUAD * PASSES * P], U32, name="x_codes", align_bytes=64)
             x_scales = codes_pool.tile([P, QUAD * PASSES * P], U8, name="x_scales", align_bytes=64)
             nc.vector.quantize_mx(
-                out=x_codes[:].bitcast(FP8X4), scales=x_scales[:], in_=grouped[q][:].rearrange("p j c -> p (j c)")
+                out=x_codes[:].bitcast(FP8X4), scales=x_scales[:], in_=grouped[q][:].rearrange("p t c -> p (t c)")
             )
             codes[q] = x_codes
             scales[q] = x_scales
 
         def mx(t):
+            if not 0 <= t < NT:
+                return
             bank = banks_mx.tile([P, GATES], F32, name="mx_bank")
-            for g in range(PASSES):
-                lo = ((t % QUAD) * PASSES + g) * P
+            for m in range(PASSES):
+                lo = ((t % QUAD) * PASSES + m) * P
                 nc.tensor.matmul_mx(
                     out=bank[:],
                     lhsT=codes[t // QUAD][:, lo:lo + P].bitcast(FP8X4),
                     lhsT_scale=scales[t // QUAD][:, lo:lo + P],
-                    rhs=w_codes[:, g, :].bitcast(FP8X4),
-                    rhs_scale=w_scales[:, g, :],
-                    start=(g == 0),
-                    stop=(g == PASSES - 1),
+                    rhs=w_codes[:, m, :].bitcast(FP8X4),
+                    rhs_scale=w_scales[:, m, :],
+                    start=(m == 0),
+                    stop=(m == PASSES - 1),
                 )
             mx_banks[t] = bank
 
         def add(t):
+            if not 0 <= t < NT:
+                return
             dst = sums[t // PAIR][:, t % PAIR, :]
             nc.vector.tensor_tensor(out=dst, in0=mx_banks[t][:], in1=dst, op=ALU.add)
 
-        def gates(u):
-            b = batch_of(u)
-            b_lo, b_n, engine = batches[b]
-            u_lo, u_n = units[u]
+        def gates(unit):
+            if not 0 <= unit < len(units):
+                return
+            b = batch_of(unit)
+            b_lo, b_n = batches[b][0:2]
+            lo, n = units[unit]
             if b not in acts:
                 act = act_pool.tile([P, b_n, GATES], F32, name="act")
                 acts[b] = act
-            dst = acts[b][:, u_lo - b_lo:u_lo - b_lo + u_n, :]
-            src = sums[u_lo // PAIR][:, u_lo % PAIR:u_lo % PAIR + u_n, :]
+            dst = acts[b][:, lo - b_lo:lo - b_lo + n, :]
+            src = sums[lo // PAIR][:, lo % PAIR:lo % PAIR + n, :]
             nc.scalar.activation(out=dst[:, :, HID:GATES], in_=src[:, :, HID:GATES], func=ACT.Sigmoid)
             nc.scalar.activation(out=dst[:, :, 0:HID], in_=src[:, :, 0:HID], func=ACT.Tanh)
 
         def prod(b):
+            if not 0 <= b < len(batches):
+                return
             b_lo, b_n, engine = batches[b]
             act = acts[b]
             if b < N_FULL:
@@ -284,6 +293,8 @@ def tile_symlstmcell_t_kernel(tc, x, h0, c0, weight_ih, weight_hh, bias_ih, bias
             )
 
         def c1(b):
+            if not 0 <= b < len(batches):
+                return
             b_lo, b_n, engine = batches[b]
             c1_sb = out_pool.tile([P, b_n, HID], F32, name="c1_sb")
             c1_tiles[b] = c1_sb
@@ -291,99 +302,69 @@ def tile_symlstmcell_t_kernel(tc, x, h0, c0, weight_ih, weight_hh, bias_ih, bias
             nc.sync.dma_start(out=c1_view[:, b_lo:b_lo + b_n, :], in_=c1_sb[:])
 
         def tanh_c(b):
+            if not 0 <= b < len(batches):
+                return
             nc.scalar.activation(out=links[b][:], in_=c1_tiles[b][:], func=ACT.Tanh)
 
         def h1(b):
-            b_lo, b_n, engine = batches[b]
+            if not 0 <= b < len(batches):
+                return
+            b_lo, b_n = batches[b][0:2]
             h1_sb = out_pool.tile([P, b_n, HID], F32, name="h1_sb")
             nc.vector.tensor_tensor(out=h1_sb[:], in0=links[b][:], in1=acts[b][:, :, 3 * HID:GATES], op=ALU.mult)
             nc.sync.dma_start(out=h1_view[:, b_lo:b_lo + b_n, :], in_=h1_sb[:])
 
-        run = {
-            "w_group": w_group, "w_quant": w_quant, "h_t": h_t, "h_out": h_out, "plain": plain, "plain_out": plain_out,
-            "x_t": x_t, "x_out": x_out, "quant": quant, "mx": mx, "add": add, "gates": gates, "prod": prod, "c1": c1,
-            "tanh_c": tanh_c, "h1": h1,
-        }
-        count = {
-            "x_t": NT, "x_out": NT, "quant": NQ, "mx": NT, "add": NT, "plain": NT, "plain_out": NT,
-            "h_t": NT // H_BLOCK, "h_out": NT // H_BLOCK, "gates": n_pairs,
-            "prod": N_FULL, "c1": N_FULL, "tanh_c": N_FULL, "h1": N_FULL,
-        }
-        per_period = {
-            "x_t": QUAD, "x_out": QUAD, "quant": 1, "mx": QUAD, "add": QUAD, "plain": QUAD, "plain_out": QUAD,
-            "gates": QUAD // PAIR, "prod": 1, "c1": 1, "tanh_c": 1, "h1": 1,
-        }
+        for m in range(PASSES):
+            w_group(m)
+        for m in range(PASSES):
+            w_quant(m)
 
-        def needs(stage, i):
-            if stage == "w_quant":
-                return [("w_group", i)]
-            if stage == "x_out":
-                return [("x_t", i)]
-            if stage == "quant":
-                return [("x_out", QUAD * i + r) for r in range(QUAD)]
-            if stage == "mx":
-                return [("quant", i // QUAD)] + [("w_quant", g) for g in range(PASSES)]
-            if stage == "add":
-                return [("mx", i), ("plain_out", i)]
-            if stage == "plain_out":
-                return [("plain", i)] + ([("plain_out", i - 1)] if i > 0 else [])
-            if stage == "plain":
-                return [("h_out", i // H_BLOCK)]
-            if stage == "h_out":
-                return [("h_t", i)]
-            if stage == "gates":
-                return [("add", t) for t in range(units[i][0], units[i][0] + units[i][1])]
-            if stage == "prod":
-                frees_slot = [("h1", i - LINK_BUFS)] if LINK_BUFS <= i < N_FULL else []
-                return [("gates", u) for u in range(len(units)) if batch_of(u) == i] + frees_slot
-            if stage == "c1":
-                return [("prod", i)]
-            if stage == "tanh_c":
-                return [("c1", i)]
-            if stage == "h1":
-                return [("tanh_c", i)]
-            return []
+        for period in range(FIRST_PERIOD, NQ):
+            now = QUAD * period
+            far = now + 2 * QUAD
+            gates(2 * period - 1)
+            if (period - FIRST_PERIOD) % 2 == 0:
+                h_t((period - FIRST_PERIOD) // 2)
+                h_out((period - FIRST_PERIOD) // 2)
+            tanh_c(period - 2)
+            h1(period - 3)
+            prod(period - 1)
+            c1(period - 1)
+            quant(period + 1)
+            mx(now)
+            mx(now + 1)
+            add(now)
+            add(now + 1)
+            plain(far)
+            x_t(far)
+            x_t(far + 1)
+            plain(far + 1)
+            plain_out(far)
+            plain_out(far + 1)
+            x_out(far)
+            x_out(far + 1)
+            x_t(far + 2)
+            x_t(far + 3)
+            x_out(far + 2)
+            gates(2 * period)
+            x_out(far + 3)
+            mx(now + 2)
+            mx(now + 3)
+            add(now + 2)
+            add(now + 3)
+            plain(far + 2)
+            plain(far + 3)
+            plain_out(far + 2)
+            plain_out(far + 3)
 
-        def expand(order, mine):
-            items = []
-            for k in range(FIRST_PERIOD, NQ):
-                for (stage, ahead, r) in order:
-                    if stage == "h_t" or stage == "h_out":
-                        if (k + ahead) % 2 == r and 0 <= (k + ahead) // 2 < count[stage]:
-                            items.append((stage, (k + ahead) // 2))
-                        continue
-                    i = per_period[stage] * (k + ahead) + r
-                    if 0 <= k + ahead and i < count[stage] and mine(stage, i):
-                        items.append((stage, i))
-            return items
-
-        weight_first = [("w_group", g) for g in range(PASSES)] + [("w_quant", g) for g in range(PASSES)]
         small = list(range(N_FULL, len(batches)))
-        vector_end = [("h1", N_FULL - 2)]
+        for unit in range(2 * NQ - 1, len(units)):
+            gates(unit)
+        h1(N_FULL - 2)
         for b in small:
-            vector_end.extend([("prod", b), ("c1", b)])
-        vector_end.extend([("h1", b) for b in [N_FULL - 1] + small])
-        scalar_end = [("gates", n_pairs + j) for j in range(len(small))] + [("tanh_c", b) for b in [N_FULL - 1] + small]
-        orders = [
-            expand(TENSOR_ORDER, lambda stage, i: True),
-            weight_first + expand(VECTOR_ORDER, lambda stage, i: stage != "plain_out" or not on_scalar(i)) + vector_end,
-            expand(SCALAR_ORDER, lambda stage, i: stage != "plain_out" or on_scalar(i)) + scalar_end,
-            expand(GPSIMD_ORDER, lambda stage, i: True),
-        ]
-
-        written = set()
-        position = [0, 0, 0, 0]
-        left = sum([len(order) for order in orders])
-        while left > 0:
-            moved = False
-            for e in range(len(orders)):
-                while position[e] < len(orders[e]):
-                    stage, i = orders[e][position[e]]
-                    if not all([item in written for item in needs(stage, i)]):
-                        break
-                    run[stage](i)
-                    written.add((stage, i))
-                    position[e] += 1
-                    left -= 1
-                    moved = True
-            assert moved, "the four orders wait for each other"
+            prod(b)
+            c1(b)
+        for b in [N_FULL - 1] + small:
+            tanh_c(b)
+        for b in [N_FULL - 1] + small:
+            h1(b)

from contextlib import ExitStack

import concourse.mybir as mybir
from concourse.masks import make_identity

F32 = mybir.dt.float32
BF16 = mybir.dt.bfloat16
U32 = mybir.dt.uint32
U8 = mybir.dt.uint8
FP8X4 = mybir.dt.float8_e4m3fn_x4
ACT = mybir.ActivationFunctionType
ALU = mybir.AluOpType

P = 128
BATCH = 8192
K_IN = 1024
HID = 128
GATES = 4 * HID
PASSES = K_IN // 512
NT = BATCH // P
QUAD = 4
NQ = NT // QUAD
PAIR = 2
H_BLOCK = 8

FLOPS = 2 * BATCH * K_IN * GATES + 2 * BATCH * HID * GATES

LAST_TILES = 4
LAST_BATCHES = [(NT - 4, 2), (NT - 2, 1), (NT - 1, 1)]
N_FULL = (NT - LAST_TILES) // QUAD

X_BUFS = 4
GROUPED_BUFS = 2
CODES_BUFS = 2
SUM_BUFS = 6
ACT_BUFS = 4
OUT_BUFS = 4
LINK_BUFS = 2
HT_BUFS = 3
BANKS_T = 4
BANKS_MX = 2
BANKS_PLAIN = 2

FIRST_PERIOD = -3


def tile_symlstmcell_t_kernel(tc, x, h0, c0, weight_ih, weight_hh, bias_ih, bias_hh, out_0, out_1):
    nc = tc.nc
    x_view = x.rearrange("(p t) k -> p t k", t=NT)
    h0_view = h0.rearrange("(p t) k -> p t k", t=NT)
    c0_view = c0.rearrange("(p t) k -> p t k", t=NT)
    h1_view = out_0.rearrange("(p t) u -> p t u", t=NT)
    c1_view = out_1.rearrange("(p t) u -> p t u", t=NT)

    with ExitStack() as ctx:
        const = ctx.enter_context(tc.tile_pool(name="const", bufs=1))
        x_pool = ctx.enter_context(tc.tile_pool(name="x_pool", bufs=X_BUFS))
        grouped_pool = ctx.enter_context(tc.tile_pool(name="grouped_pool", bufs=GROUPED_BUFS))
        codes_pool = ctx.enter_context(tc.tile_pool(name="codes_pool", bufs=CODES_BUFS))
        sum_pool = ctx.enter_context(tc.tile_pool(name="sum_pool", bufs=SUM_BUFS))
        act_pool = ctx.enter_context(tc.tile_pool(name="act_pool", bufs=ACT_BUFS))
        out_pool = ctx.enter_context(tc.tile_pool(name="out_pool", bufs=OUT_BUFS))
        link_pool = ctx.enter_context(tc.tile_pool(name="link_pool", bufs=LINK_BUFS))
        last_pool = ctx.enter_context(tc.tile_pool(name="last_pool", bufs=len(LAST_BATCHES)))
        ht_pool = ctx.enter_context(tc.tile_pool(name="ht_pool", bufs=HT_BUFS))
        banks_t = ctx.enter_context(tc.psum_pool(name="banks_t", bufs=BANKS_T))
        banks_mx = ctx.enter_context(tc.psum_pool(name="banks_mx", bufs=BANKS_MX))
        banks_plain = ctx.enter_context(tc.psum_pool(name="banks_plain", bufs=BANKS_PLAIN))
        ctx.enter_context(tc.manual_schedule())

        ident_f32 = const.tile([P, P], F32, name="ident_f32")
        ident_bf16 = const.tile([P, P], BF16, name="ident_bf16")
        make_identity(nc, ident_bf16[:])
        make_identity(nc, ident_f32[:])
        bias_rows = const.tile([P, GATES], BF16, name="bias_rows")
        nc.vector.memset(bias_rows[:], 0.0)
        ones = const.tile([P, P], BF16, name="ones")
        nc.vector.memset(ones[:], 1.0)
        warm = const.tile([P, 1], F32, name="warm")
        nc.vector.memset(warm[:], 0.0)
        nc.sync.dma_start(out=bias_rows[0:1, :], in_=bias_ih.rearrange("(o n) -> o n", o=1))
        nc.scalar.dma_start(out=bias_rows[1:2, :], in_=bias_hh.rearrange("(o n) -> o n", o=1))
        nc.scalar.activation(out=warm[:], in_=warm[:], func=ACT.Sigmoid)

        h0_parts = []
        c0_parts = []
        x_tiles = {}

        def load_part(parts, view, lo, hi, label):
            part = const.tile([P, hi - lo, HID], BF16, name="%s%d" % (label, lo))
            nc.sync.dma_start(out=part[:], in_=view[:, lo:hi, :])
            parts.append((lo, hi, part))

        def part_of(parts, lo, n):
            found = [(first, part) for (first, end, part) in parts if first <= lo and lo + n <= end]
            assert len(found) == 1
            first, part = found[0]
            return part[:, lo - first:lo - first + n, :]

        def load_x(q):
            x_sb = x_pool.tile([P, QUAD, K_IN], BF16, name="x_sb")
            nc.sync.dma_start(out=x_sb[:], in_=x_view[:, QUAD * q:QUAD * (q + 1), :])
            x_tiles[q] = x_sb

        w_raw = const.tile([P, PASSES * 4 * GATES], BF16, name="w_raw")
        nc.sync.dma_start(
            out=w_raw[:].rearrange("p (a n) -> p a n", a=2 * PASSES),
            in_=weight_ih.rearrange("(a p e) c -> p a (e c)", a=2 * PASSES, e=2),
        )
        load_part(h0_parts, h0_view, 0, 8, "h0_")
        w_hh = const.tile([P, GATES], BF16, name="w_hh")
        nc.sync.dma_start(out=w_hh[:], in_=weight_hh)
        load_x(0)
        load_part(h0_parts, h0_view, 8, 24, "h0_")
        load_x(1)
        load_part(c0_parts, c0_view, 0, 16, "c0_")
        load_x(2)
        load_part(h0_parts, h0_view, 24, NT, "h0_")
        load_x(3)
        load_part(c0_parts, c0_view, 16, NT, "c0_")

        bias_bank = banks_plain.tile([P, GATES], F32, name="plain_bank")
        nc.tensor.matmul(out=bias_bank[:], lhsT=ones[:], rhs=bias_rows[:], start=True, stop=True)
        bias_all = const.tile([P, GATES], F32, name="bias_all")
        nc.scalar.copy(out=bias_all[:], in_=bias_bank[:])
        w_view = w_raw[:].rearrange("p (m v c) -> p m v c", m=PASSES, v=4)
        w_codes = const.tile([P, PASSES, GATES], U32, name="w_codes", align_bytes=64)
        w_scales = const.tile([P, PASSES, GATES], U8, name="w_scales", align_bytes=64)
        w_grouped = [
            const.tile([P, GATES, 4], BF16, name="w_grouped%d" % m, align_bytes=64) for m in range(PASSES)
        ]

        units = [(PAIR * j, PAIR) for j in range(N_FULL * QUAD // PAIR)] + LAST_BATCHES
        batches = [(QUAD * b, QUAD, nc.gpsimd) for b in range(N_FULL)] + [(lo, n, nc.vector) for (lo, n) in LAST_BATCHES]
        n_pairs = N_FULL * QUAD // PAIR

        def batch_of(unit):
            return unit * PAIR // QUAD if unit < n_pairs else N_FULL + unit - n_pairs

        def on_scalar(t):
            return t % QUAD == QUAD - 1

        h_banks = {}
        h_t_tiles = {}
        x_banks = {}
        grouped = {}
        codes = {}
        scales = {}
        plain_banks = {}
        mx_banks = {}
        sums = {}
        acts = {}
        links = {}
        c1_tiles = {}

        def w_group(m):
            nc.vector.tensor_copy(
                out=w_grouped[m][:].rearrange("p (c i) v -> p c v i", i=4),
                in_=w_view[:, m].rearrange("p v (c i) -> p c v i", i=4),
            )

        def w_quant(m):
            nc.vector.quantize_mx(
                out=w_codes[:, m, :].bitcast(FP8X4),
                scales=w_scales[:, m, :],
                in_=w_grouped[m][:].rearrange("p c v -> p (c v)"),
            )

        def h_t(b):
            if not 0 <= b < NT // H_BLOCK:
                return
            bank = banks_t.tile([P, H_BLOCK, HID], BF16, name="t_bank")
            block = part_of(h0_parts, H_BLOCK * b, H_BLOCK)
            for j in range(H_BLOCK):
                nc.tensor.transpose(bank[:, j, :], block[:, j, :], ident_bf16[:])
            h_banks[b] = bank

        def h_out(b):
            if not 0 <= b < NT // H_BLOCK:
                return
            h_t_sb = ht_pool.tile([P, H_BLOCK, HID], BF16, name="h_t_sb")
            nc.scalar.copy(out=h_t_sb[:], in_=h_banks[b][:])
            h_t_tiles[b] = h_t_sb

        def plain(t):
            if not 0 <= t < NT:
                return
            bank = banks_plain.tile([P, GATES], F32, name="plain_bank")
            with_bias = on_scalar(t)
            nc.tensor.matmul(
                out=bank[:], lhsT=h_t_tiles[t // H_BLOCK][:, t % H_BLOCK, :], rhs=w_hh[:], start=True, stop=not with_bias
            )
            if with_bias:
                nc.tensor.matmul(out=bank[:], lhsT=ones[:], rhs=bias_rows[:], start=False, stop=True)
            plain_banks[t] = bank

        def plain_out(t):
            if not 0 <= t < NT:
                return
            if t // PAIR not in sums:
                gate_sum = sum_pool.tile([P, PAIR, GATES], F32, name="gate_sum")
                sums[t // PAIR] = gate_sum
            dst = sums[t // PAIR][:, t % PAIR, :]
            if on_scalar(t):
                nc.scalar.copy(out=dst, in_=plain_banks[t][:])
            else:
                nc.vector.tensor_tensor(out=dst, in0=plain_banks[t][:], in1=bias_all[:], op=ALU.add)

        def x_t(t):
            if not 0 <= t < NT:
                return
            bank = banks_t.tile([P, 2 * PASSES, P], F32, name="t_bank")
            words = x_tiles[t // QUAD][:, t % QUAD, :].bitcast(F32)
            for a in range(2 * PASSES):
                nc.tensor.transpose(bank[:, a, :], words[:, P * a:P * (a + 1)], ident_f32[:])
            x_banks[t] = bank
            if t % QUAD == QUAD - 1 and t // QUAD + X_BUFS < NQ:
                load_x(t // QUAD + X_BUFS)

        def x_out(t):
            if not 0 <= t < NT:
                return
            q = t // QUAD
            if q not in grouped:
                x_grouped = grouped_pool.tile([P, QUAD, K_IN], BF16, name="x_grouped", align_bytes=64)
                grouped[q] = x_grouped
            nc.scalar.copy(
                out=grouped[q][:, t % QUAD, :].bitcast(F32).rearrange("p (m r u) -> p m r u", m=PASSES, u=2),
                in_=x_banks[t][:].rearrange("p (m u) r -> p m r u", u=2),
            )

        def quant(q):
            if not 0 <= q < NQ:
                return
            x_codes = codes_pool.tile([P, QUAD * PASSES * P], U32, name="x_codes", align_bytes=64)
            x_scales = codes_pool.tile([P, QUAD * PASSES * P], U8, name="x_scales", align_bytes=64)
            nc.vector.quantize_mx(
                out=x_codes[:].bitcast(FP8X4), scales=x_scales[:], in_=grouped[q][:].rearrange("p t c -> p (t c)")
            )
            codes[q] = x_codes
            scales[q] = x_scales

        def mx(t):
            if not 0 <= t < NT:
                return
            bank = banks_mx.tile([P, GATES], F32, name="mx_bank")
            for m in range(PASSES):
                lo = ((t % QUAD) * PASSES + m) * P
                nc.tensor.matmul_mx(
                    out=bank[:],
                    lhsT=codes[t // QUAD][:, lo:lo + P].bitcast(FP8X4),
                    lhsT_scale=scales[t // QUAD][:, lo:lo + P],
                    rhs=w_codes[:, m, :].bitcast(FP8X4),
                    rhs_scale=w_scales[:, m, :],
                    start=(m == 0),
                    stop=(m == PASSES - 1),
                )
            mx_banks[t] = bank

        def add(t):
            if not 0 <= t < NT:
                return
            dst = sums[t // PAIR][:, t % PAIR, :]
            nc.vector.tensor_tensor(out=dst, in0=mx_banks[t][:], in1=dst, op=ALU.add)

        def gates(unit):
            if not 0 <= unit < len(units):
                return
            b = batch_of(unit)
            b_lo, b_n = batches[b][0:2]
            lo, n = units[unit]
            if b not in acts:
                act = act_pool.tile([P, b_n, GATES], F32, name="act")
                acts[b] = act
            dst = acts[b][:, lo - b_lo:lo - b_lo + n, :]
            src = sums[lo // PAIR][:, lo % PAIR:lo % PAIR + n, :]
            nc.scalar.activation(out=dst[:, :, HID:GATES], in_=src[:, :, HID:GATES], func=ACT.Sigmoid)
            nc.scalar.activation(out=dst[:, :, 0:HID], in_=src[:, :, 0:HID], func=ACT.Tanh)

        def prod(b):
            if not 0 <= b < len(batches):
                return
            b_lo, b_n, engine = batches[b]
            act = acts[b]
            if b < N_FULL:
                link = link_pool.tile([P, b_n, HID], F32, name="link")
            else:
                link = last_pool.tile([P, b_n, HID], F32, name="last_link")
            links[b] = link
            engine.tensor_tensor(out=link[:], in0=act[:, :, 0:HID], in1=act[:, :, HID:2 * HID], op=ALU.mult)
            engine.tensor_tensor(
                out=act[:, :, 2 * HID:3 * HID], in0=act[:, :, 2 * HID:3 * HID], in1=part_of(c0_parts, b_lo, b_n), op=ALU.mult
            )

        def c1(b):
            if not 0 <= b < len(batches):
                return
            b_lo, b_n, engine = batches[b]
            c1_sb = out_pool.tile([P, b_n, HID], F32, name="c1_sb")
            c1_tiles[b] = c1_sb
            engine.tensor_tensor(out=c1_sb[:], in0=links[b][:], in1=acts[b][:, :, 2 * HID:3 * HID], op=ALU.add)
            nc.sync.dma_start(out=c1_view[:, b_lo:b_lo + b_n, :], in_=c1_sb[:])

        def tanh_c(b):
            if not 0 <= b < len(batches):
                return
            nc.scalar.activation(out=links[b][:], in_=c1_tiles[b][:], func=ACT.Tanh)

        def h1(b):
            if not 0 <= b < len(batches):
                return
            b_lo, b_n = batches[b][0:2]
            h1_sb = out_pool.tile([P, b_n, HID], F32, name="h1_sb")
            nc.vector.tensor_tensor(out=h1_sb[:], in0=links[b][:], in1=acts[b][:, :, 3 * HID:GATES], op=ALU.mult)
            nc.sync.dma_start(out=h1_view[:, b_lo:b_lo + b_n, :], in_=h1_sb[:])

        for m in range(PASSES):
            w_group(m)
        for m in range(PASSES):
            w_quant(m)

        for period in range(FIRST_PERIOD, NQ):
            now = QUAD * period
            far = now + 2 * QUAD
            gates(2 * period - 1)
            if (period - FIRST_PERIOD) % 2 == 0:
                h_t((period - FIRST_PERIOD) // 2)
                h_out((period - FIRST_PERIOD) // 2)
            tanh_c(period - 2)
            h1(period - 3)
            prod(period - 1)
            c1(period - 1)
            quant(period + 1)
            mx(now)
            mx(now + 1)
            add(now)
            add(now + 1)
            plain(far)
            x_t(far)
            x_t(far + 1)
            plain(far + 1)
            plain_out(far)
            plain_out(far + 1)
            x_out(far)
            x_out(far + 1)
            x_t(far + 2)
            x_t(far + 3)
            x_out(far + 2)
            gates(2 * period)
            x_out(far + 3)
            mx(now + 2)
            mx(now + 3)
            add(now + 2)
            add(now + 3)
            plain(far + 2)
            plain(far + 3)
            plain_out(far + 2)
            plain_out(far + 3)

        small = list(range(N_FULL, len(batches)))
        for unit in range(2 * NQ - 1, len(units)):
            gates(unit)
        h1(N_FULL - 2)
        for b in small:
            prod(b)
            c1(b)
        for b in [N_FULL - 1] + small:
            tanh_c(b)
        for b in [N_FULL - 1] + small:
            h1(b)
